import numpy as np
import ml_dtypes


def mxq(x, axis, fmt="e4m3"):
    dtype, down = {"e4m3": (ml_dtypes.float8_e4m3fn, 7), "e5m2": (ml_dtypes.float8_e5m2, 14)}[fmt]
    v = np.moveaxis(np.asarray(x, np.float32).astype(ml_dtypes.bfloat16).astype(np.float64), axis, -1)
    blocks = v.reshape(v.shape[:-1] + (-1, 32))
    amax = np.abs(blocks).max(-1, keepdims=True)
    byte = np.maximum(np.where(amax > 0, np.frexp(amax)[1] - 1 + 127, 0) - down, 1)
    scale = np.exp2(byte - 127.0)
    codes = (blocks / scale).astype(np.float32).astype(dtype).astype(np.float64)
    return np.moveaxis((codes * scale).reshape(v.shape), -1, axis)


WIDE = False


def mx_kscale(k):
    if not WIDE:
        return np.ones(k)
    levels = np.array([20, -20, 10, -10, 0])
    a = np.random.permutation(np.resize(levels, k // 512 * 4)).reshape(k // 512, 4)
    idx = np.arange(k)
    return np.exp2(a[idx // 512, idx % 128 // 32])


BF16 = ml_dtypes.bfloat16


def bf(x):
    return np.asarray(x, np.float32).astype(BF16)


def f64(x):
    return np.asarray(x).astype(np.float64)


C, S, L, D, NK = 16, 1024, 3, 32, 96
K = NK // L


def convs(Ec, Ws, bs):
    E = np.transpose(Ec, (1, 0, 2, 3))
    res = []
    for h in range(1, L + 1):
        P = L - h + 1
        win = np.stack([E[:, :, p:p + h, :] for p in range(P)], axis=0).reshape(P * S, C * h * D)
        z = win @ Ws[h - 1].reshape(K * C, C * h * D).T + bs[h - 1].reshape(1, K * C)
        res.append(z.reshape(P, S, K, C))
    return res


def setup_inputs():
    u = mx_kscale(K * C).reshape(K, C)
    Ec = bf(np.random.standard_normal((C, S, L, D)))
    W0 = [bf(np.random.standard_normal((K, C, C, h, D)) / np.sqrt(C * h * D)) for h in range(1, L + 1)]
    bs = [bf(np.random.standard_normal((K, C)) * 0.3) for h in range(1, L + 1)]
    ug = np.repeat(u.T, L, axis=1)
    g = np.random.standard_normal((C, S, 1, NK)) * np.exp2(np.random.randint(-12, 1, (1, S, 1, 1))) * 4.0
    g = bf(g * ug[:, None, None, :])
    zs = convs(f64(Ec), [f64(w) for w in W0], [f64(b) for b in bs])
    inp = {'Ec': Ec}
    for h in range(1, L + 1):
        inp['W%d' % h] = bf(f64(W0[h - 1]) / u[:, :, None, None, None])
    for h in range(1, L + 1):
        inp['b%d' % h] = bs[h - 1]
    for h in range(1, L + 1):
        inp['conv%d' % h] = np.asarray(zs[h - 1], np.float32)
    inp['grad_out'] = g
    return inp


def reference(Ec, W1, W2, W3, b1, b2, b3, conv1, conv2, conv3, grad_out):
    g = f64(grad_out)[:, :, 0, :]
    Ws = [f64(W1), f64(W2), f64(W3)]
    zs = [f64(conv1), f64(conv2), f64(conv3)]
    acc = np.zeros((S, C, L, D))
    for h in range(1, L + 1):
        P = L - h + 1
        z = zs[h - 1]
        gh = np.transpose(g[:, :, h - 1::L], (1, 2, 0))
        m = np.max(z, axis=0)
        hit = (z == m[None]) * 1.0
        n = np.sum(hit, axis=0)
        dz = gh[None] * hit * (((m > 0.0) * 1.0) / n)[None]
        d = mxq(dz.reshape(P * S, K * C), 1, 'e5m2') @ mxq(Ws[h - 1].reshape(K * C, C * h * D), 0, 'e4m3')
        d = d.reshape(P, S, C, h, D)
        for p in range(P):
            acc[:, :, p:p + h, :] = acc[:, :, p:p + h, :] + d[p]
    return np.transpose(acc, (1, 0, 2, 3))

@@ -1,0 +1,258 @@
+from contextlib import ExitStack
+
+from concourse import mybir
+from concourse.masks import make_identity
+
+F32 = mybir.dt.float32
+BF16 = mybir.dt.bfloat16
+U32 = mybir.dt.uint32
+U8 = mybir.dt.uint8
+E4M3_X4 = mybir.dt.float8_e4m3fn_x4
+E5M2_X4 = mybir.dt.float8_e5m2_x4
+ALU = mybir.AluOpType
+ACT = mybir.ActivationFunctionType
+
+P = 128
+C_CH = 16
+S = 1024
+L = 3
+D = 32
+J = 32
+K = J * C_CH
+N_COLS = C_CH * D
+TILES = S // P
+GT = 2
+GROUPS = TILES // GT
+GC = GT * K
+WORDS = K // 2
+SMALLEST_NORMAL = 2.0**-126
+
+FLOPS = 2 * K * S * N_COLS * (3 * 1 + 2 * 2 + 1 * 3)
+BYTES = 4 * 6 * S * K + 2 * C_CH * S * 96 + 2 * K * N_COLS * 6 + 4 * C_CH * S * L * D
+
+
+def first_weight_slot(h):
+    return h * (h - 1) // 2
+
+
+def tile_vrtconv_t_v_kernel(
+    tc, Ec, W1, W2, W3, b1, b2, b3, conv1, conv2, conv3, grad_out, out
+):
+    nc = tc.nc
+    weights = {1: W1, 2: W2, 3: W3}
+
+    conv_views = {
+        1: conv1.rearrange("q (p t) j o -> p q t (j o)", t=TILES),
+        2: conv2.rearrange("q (p t) j o -> p q t (j o)", t=TILES),
+        3: conv3.rearrange("q (p t) j o -> p q t (j o)", t=TILES),
+    }
+    grad_view = grad_out.rearrange("o (p t) x i -> p o t (x i)", t=TILES)
+    out_view = out.rearrange("c (p t) l d -> p c t (l d)", t=TILES)
+
+    with ExitStack() as stack:
+        keep = stack.enter_context(tc.tile_pool(name="keep", bufs=1))
+        wstage = stack.enter_context(tc.tile_pool(name="wstage", bufs=2))
+        loads = stack.enter_context(tc.tile_pool(name="loads", bufs=2))
+        work = stack.enter_context(tc.tile_pool(name="work", bufs=2))
+        acc_pool = stack.enter_context(tc.psum_pool(name="acc", bufs=1))
+        xt_pool = stack.enter_context(tc.psum_pool(name="xt", bufs=4))
+        cnt_pool = stack.enter_context(tc.psum_pool(name="cnt", bufs=1))
+
+        ident_f32 = keep.tile([P, P], F32)
+        make_identity(nc, ident_f32[:])
+        ident_bf16 = keep.tile([P, P], BF16)
+        make_identity(nc, ident_bf16[:])
+
+        w_codes = keep.tile([P, 6, N_COLS], U32, align_bytes=64)
+        w_scales = keep.tile([P, 6, N_COLS], U8, align_bytes=64)
+
+        def load_group(g):
+            tiles_of_g = slice(g * GT, (g + 1) * GT)
+            z = {}
+            for h in (1, 2, 3):
+                z[h] = loads.tile([P, L - h + 1, GT, K], F32, name="z%d" % h)
+                nc.sync.dma_start(out=z[h][:], in_=conv_views[h][:, :, tiles_of_g, :])
+            g_raw = loads.tile([P, C_CH, GT, J, L], BF16, name="g_raw")
+            nc.sync.dma_start(
+                out=g_raw[:].rearrange("p o t j h -> p o t (j h)"),
+                in_=grad_view[:, :, tiles_of_g, :],
+            )
+            return z, g_raw
+
+        def load_weights():
+            w_raw = {}
+            for h in (1, 2, 3):
+                w_raw[h] = keep.tile([P, 4, h * N_COLS], BF16, name="w_raw%d" % h)
+                rows = weights[h].rearrange("j o c a d -> (j o) (c a d)")
+                nc.sync.dma_start(
+                    out=w_raw[h][:].rearrange("p (u e) n -> p u (e n)", u=2),
+                    in_=rows.rearrange("(u p e) n -> p u (e n)", u=2, e=2),
+                )
+            return w_raw
+
+        def quantise_weights(w_raw):
+            for h in (1, 2, 3):
+                by_row = w_raw[h][:].rearrange("p t (c a d) -> p a c d t", a=h, d=D)
+                for a in range(h):
+                    w_grouped = wstage.tile([P, C_CH, D, 4], BF16, align_bytes=64)
+                    nc.scalar.copy(out=w_grouped[:], in_=by_row[:, a])
+                    slot = first_weight_slot(h) + a
+                    nc.vector.quantize_mx(
+                        out=w_codes[:, slot, :].bitcast(E4M3_X4),
+                        scales=w_scales[:, slot, :],
+                        in_=w_grouped[:].rearrange("p c d t -> p (c d t)"),
+                    )
+
+        def sort_grad(g_raw):
+            g_sorted = work.tile([P, L, GT, K], BF16)
+            for h in range(L):
+                for t in range(GT):
+                    nc.scalar.copy(
+                        out=g_sorted[:, h, t, :].rearrange("p (b i o) -> p b o i", i=4, o=C_CH),
+                        in_=g_raw[:, :, t, :, h].rearrange("p o (b i) -> p b o i", i=4),
+                    )
+            return g_sorted
+
+        def hits(z, g_sorted):
+            z1 = z[1][:].rearrange("p q t k -> p q (t k)")
+            z2 = z[2][:].rearrange("p q t k -> p q (t k)")
+            z3 = z[3][:].rearrange("p q t k -> p (q t k)")
+            g3 = g_sorted[:, 2].rearrange("p t k -> p (t k)")
+            dz_a = work.tile([P, 4, GT, K], BF16)
+            dz_b = work.tile([P, 2, GT, K], BF16)
+            a_planes = dz_a[:].rearrange("p q t k -> p q (t k)")
+            b_planes = dz_b[:].rearrange("p q t k -> p q (t k)")
+
+            top = work.tile([P, GC], F32)
+            nc.vector.scalar_tensor_tensor(
+                out=top[:], in0=z1[:, 0], scalar=SMALLEST_NORMAL, in1=z1[:, 1],
+                op0=ALU.max, op1=ALU.max,
+            )
+            nc.vector.scalar_tensor_tensor(
+                out=b_planes[:, 0], in0=z2[:, 1], scalar=SMALLEST_NORMAL, in1=z2[:, 0],
+                op0=ALU.max, op1=ALU.is_le,
+            )
+            nc.vector.tensor_tensor(out=top[:], in0=top[:], in1=z1[:, 2], op=ALU.max)
+            nc.vector.scalar_tensor_tensor(
+                out=b_planes[:, 1], in0=z2[:, 0], scalar=SMALLEST_NORMAL, in1=z2[:, 1],
+                op0=ALU.max, op1=ALU.is_le,
+            )
+            nc.vector.tensor_tensor(
+                out=a_planes[:, 0:3], in0=z1,
+                in1=top[:].unsqueeze(1).to_broadcast([P, 3, GC]), op=ALU.is_ge,
+            )
+            nc.vector.scalar_tensor_tensor(
+                out=a_planes[:, 3], in0=z3, scalar=0.0, in1=g3, op0=ALU.is_gt, op1=ALU.mult,
+            )
+            return dz_a, dz_b
+
+        def share_and_mask(dz_a, dz_b, g_sorted):
+            a_planes = dz_a[:].rearrange("p q t k -> p q (t k)")
+            b_planes = dz_b[:].rearrange("p q t k -> p q (t k)")
+            g1 = g_sorted[:, 0].rearrange("p t k -> p (t k)")
+            g2 = g_sorted[:, 1].rearrange("p t k -> p (t k)")
+
+            share1 = work.tile([P, GT, K], BF16)
+            for t in range(GT):
+                count = cnt_pool.tile([P, K], F32)
+                for q in range(3):
+                    nc.tensor.matmul(
+                        out=count[:], lhsT=ident_bf16[:], rhs=dz_a[:, q, t, :],
+                        start=(q == 0), stop=(q == 2),
+                    )
+                nc.scalar.activation(
+                    out=share1[:, t, :], in_=count[:], func=ACT.Copy, scale=-0.5, bias=1.5
+                )
+            share2 = work.tile([P, GC], BF16)
+            nc.vector.tensor_tensor(
+                out=share2[:], in0=b_planes[:, 0], in1=b_planes[:, 1], op=ALU.add
+            )
+            nc.vector.tensor_scalar(
+                out=share2[:], in0=share2[:], scalar1=-0.5, scalar2=1.5, op0=ALU.mult, op1=ALU.add
+            )
+            nc.vector.tensor_tensor(out=share2[:], in0=share2[:], in1=g2, op=ALU.mult)
+            flat1 = share1[:].rearrange("p t k -> p (t k)")
+            nc.vector.scalar_tensor_tensor(
+                out=flat1, in0=flat1, scalar=1.0 / 3.0, in1=g1, op0=ALU.max, op1=ALU.mult
+            )
+            nc.vector.tensor_tensor(
+                out=b_planes, in0=b_planes,
+                in1=share2[:].unsqueeze(1).to_broadcast([P, 2, GC]), op=ALU.mult,
+            )
+            nc.vector.tensor_tensor(
+                out=a_planes[:, 0:3], in0=a_planes[:, 0:3],
+                in1=flat1.unsqueeze(1).to_broadcast([P, 3, GC]), op=ALU.mult,
+            )
+
+        def transpose_and_quantise(dz, planes, label):
+            slots = GT * planes
+            grouped = work.tile([P, slots, P, 4], BF16, align_bytes=64, name="grouped" + label)
+            grouped_words = grouped[:].bitcast(F32)
+            for pair in range(slots // 2):
+                xt = xt_pool.tile([P, 2, 2, P], F32)
+                for i in range(2):
+                    t, q = divmod(2 * pair + i, planes)
+                    words = dz[:, q, t, :].bitcast(F32)
+                    for u in range(2):
+                        nc.tensor.transpose(
+                            out=xt[:, i, u, :], in_=words[:, u * P : (u + 1) * P],
+                            identity=ident_f32[:],
+                        )
+                nc.scalar.copy(
+                    out=grouped_words[:, 2 * pair : 2 * pair + 2],
+                    in_=xt[:].rearrange("p i u s -> p i s u"),
+                )
+            codes = work.tile([P, slots, P], U32, align_bytes=64, name="codes" + label)
+            scales = work.tile([P, slots, P], U8, align_bytes=64, name="scales" + label)
+            nc.vector.quantize_mx(
+                out=codes[:].rearrange("p n s -> p (n s)").bitcast(E5M2_X4),
+                scales=scales[:].rearrange("p n s -> p (n s)"),
+                in_=grouped[:].rearrange("p n s t -> p (n s t)"),
+            )
+            return codes, scales
+
+        def multiply_and_store(g, quantised_a, quantised_b):
+            staged = work.tile([P, C_CH, GT, L, D], F32)
+            for t in range(GT):
+                acc = [acc_pool.tile([P, N_COLS], F32, name="acc%d" % l) for l in range(L)]
+                for h in (1, 2, 3):
+                    for p in range(L - h + 1):
+                        if h == 2:
+                            (codes, scales), slot = quantised_b, t * 2 + p
+                        else:
+                            (codes, scales), slot = quantised_a, t * 4 + (p if h == 1 else 3)
+                        for a in range(h):
+                            w_slot = first_weight_slot(h) + a
+                            nc.tensor.matmul_mx(
+                                out=acc[p + a][:],
+                                lhsT=codes[:, slot, :].bitcast(E5M2_X4),
+                                lhsT_scale=scales[:, slot, :],
+                                rhs=w_codes[:, w_slot, :].bitcast(E4M3_X4),
+                                rhs_scale=w_scales[:, w_slot, :],
+                                start=(h == 1),
+                                stop=(h == 3),
+                            )
+                for l in range(L):
+                    nc.scalar.copy(
+                        out=staged[:, :, t, l, :],
+                        in_=acc[l][:].rearrange("p (c d) -> p c d", d=D),
+                    )
+            nc.sync.dma_start(
+                out=out_view[:, :, g * GT : (g + 1) * GT, :],
+                in_=staged[:].rearrange("p c t l d -> p c t (l d)"),
+            )
+
+        loaded = load_group(0)
+        w_raw = load_weights()
+        for g in range(GROUPS):
+            z, g_raw = loaded
+            if g + 1 < GROUPS:
+                loaded = load_group(g + 1)
+            g_sorted = sort_grad(g_raw)
+            dz_a, dz_b = hits(z, g_sorted)
+            share_and_mask(dz_a, dz_b, g_sorted)
+            if g == 0:
+                quantise_weights(w_raw)
+            quantised_a = transpose_and_quantise(dz_a, 4, "A")
+            quantised_b = transpose_and_quantise(dz_b, 2, "B")
+            multiply_and_store(g, quantised_a, quantised_b)

@@ -21,14 +21,15 @@ J = 32
 K = J * C_CH
 N_COLS = C_CH * D
 TILES = S // P
-GT = 2
-GROUPS = TILES // GT
-GC = GT * K
-WORDS = K // 2
+GROUP_TILES = (1, 1, 2, 2, 1, 1)
+GROUPS = len(GROUP_TILES)
 SMALLEST_NORMAL = 2.0**-126
+PASSES = [(h, p, a) for h in (2, 1, 3) for p in range(L - h + 1) for a in range(h)]
 
-FLOPS = 2 * K * S * N_COLS * (3 * 1 + 2 * 2 + 1 * 3)
+FLOPS = 2 * K * S * N_COLS * len(PASSES)
 BYTES = 4 * 6 * S * K + 2 * C_CH * S * 96 + 2 * K * N_COLS * 6 + 4 * C_CH * S * L * D
+
+assert sum(GROUP_TILES) == TILES
 
 
 def first_weight_slot(h):
@@ -49,81 +50,91 @@ def tile_vrtconv_t_v_kernel(
     grad_view = grad_out.rearrange("o (p t) x i -> p o t (x i)", t=TILES)
     out_view = out.rearrange("c (p t) l d -> p c t (l d)", t=TILES)
 
+    def tiles_of(g):
+        first = sum(GROUP_TILES[:g])
+        return slice(first, first + GROUP_TILES[g])
+
     with ExitStack() as stack:
         keep = stack.enter_context(tc.tile_pool(name="keep", bufs=1))
-        wstage = stack.enter_context(tc.tile_pool(name="wstage", bufs=2))
+        wstage = stack.enter_context(tc.tile_pool(name="wstage", bufs=3))
         loads = stack.enter_context(tc.tile_pool(name="loads", bufs=2))
         work = stack.enter_context(tc.tile_pool(name="work", bufs=2))
         acc_pool = stack.enter_context(tc.psum_pool(name="acc", bufs=1))
         xt_pool = stack.enter_context(tc.psum_pool(name="xt", bufs=4))
         cnt_pool = stack.enter_context(tc.psum_pool(name="cnt", bufs=1))
+        stack.enter_context(tc.manual_schedule())
 
         ident_f32 = keep.tile([P, P], F32)
         make_identity(nc, ident_f32[:])
         ident_bf16 = keep.tile([P, P], BF16)
         make_identity(nc, ident_bf16[:])
 
+        w_raw = {}
+        w_grouped = {}
         w_codes = keep.tile([P, 6, N_COLS], U32, align_bytes=64)
         w_scales = keep.tile([P, 6, N_COLS], U8, align_bytes=64)
 
+        z_of, g_raw_of, g_sorted_of, dz_of, share1_of, share2_of, grouped_of, quantised_of = (
+            {}, {}, {}, {}, {}, {}, {}, {},
+        )
+
         def load_group(g):
-            tiles_of_g = slice(g * GT, (g + 1) * GT)
-            z = {}
-            for h in (1, 2, 3):
-                z[h] = loads.tile([P, L - h + 1, GT, K], F32, name="z%d" % h)
-                nc.sync.dma_start(out=z[h][:], in_=conv_views[h][:, :, tiles_of_g, :])
-            g_raw = loads.tile([P, C_CH, GT, J, L], BF16, name="g_raw")
+            gt = GROUP_TILES[g]
+            z = {h: loads.tile([P, L - h + 1, gt, K], F32, name="z%d" % h) for h in (1, 2, 3)}
+            g_raw = loads.tile([P, C_CH, gt, J, L], BF16, name="g_raw")
+            for h in (1, 2):
+                nc.sync.dma_start(out=z[h][:], in_=conv_views[h][:, :, tiles_of(g), :])
             nc.sync.dma_start(
                 out=g_raw[:].rearrange("p o t j h -> p o t (j h)"),
-                in_=grad_view[:, :, tiles_of_g, :],
+                in_=grad_view[:, :, tiles_of(g), :],
             )
-            return z, g_raw
+            nc.sync.dma_start(out=z[3][:], in_=conv_views[3][:, :, tiles_of(g), :])
+            z_of[g], g_raw_of[g] = z, g_raw
 
-        def load_weights():
-            w_raw = {}
-            for h in (1, 2, 3):
-                w_raw[h] = keep.tile([P, 4, h * N_COLS], BF16, name="w_raw%d" % h)
-                rows = weights[h].rearrange("j o c a d -> (j o) (c a d)")
-                nc.sync.dma_start(
-                    out=w_raw[h][:].rearrange("p (u e) n -> p u (e n)", u=2),
-                    in_=rows.rearrange("(u p e) n -> p u (e n)", u=2, e=2),
-                )
-            return w_raw
+        def load_weight(h):
+            w_raw[h] = keep.tile([P, 4, h * N_COLS], BF16, name="w_raw%d" % h)
+            rows = weights[h].rearrange("j o c a d -> (j o) (c a d)")
+            nc.sync.dma_start(
+                out=w_raw[h][:].rearrange("p (u e) n -> p u (e n)", u=2),
+                in_=rows.rearrange("(u p e) n -> p u (e n)", u=2, e=2),
+            )
 
-        def quantise_weights(w_raw):
-            for h in (1, 2, 3):
+        def regroup_weights(heights):
+            for h in heights:
                 by_row = w_raw[h][:].rearrange("p t (c a d) -> p a c d t", a=h, d=D)
                 for a in range(h):
-                    w_grouped = wstage.tile([P, C_CH, D, 4], BF16, align_bytes=64)
-                    nc.scalar.copy(out=w_grouped[:], in_=by_row[:, a])
-                    slot = first_weight_slot(h) + a
+                    grouped = wstage.tile([P, C_CH, D, 4], BF16, align_bytes=64, name="w_grouped")
+                    nc.scalar.copy(out=grouped[:], in_=by_row[:, a])
+                    w_grouped[first_weight_slot(h) + a] = grouped
+
+        def quantise_weights(heights):
+            for h in heights:
+                for slot in range(first_weight_slot(h), first_weight_slot(h) + h):
                     nc.vector.quantize_mx(
                         out=w_codes[:, slot, :].bitcast(E4M3_X4),
                         scales=w_scales[:, slot, :],
-                        in_=w_grouped[:].rearrange("p c d t -> p (c d t)"),
+                        in_=w_grouped[slot][:].rearrange("p c d t -> p (c d t)"),
                     )
 
-        def sort_grad(g_raw):
-            g_sorted = work.tile([P, L, GT, K], BF16)
-            for h in range(L):
-                for t in range(GT):
+        def sort_grad(g):
+            g_sorted = work.tile([P, L, GROUP_TILES[g], K], BF16, name="g_sorted")
+            for h in (3, 2, 1):
+                for t in range(GROUP_TILES[g]):
                     nc.scalar.copy(
-                        out=g_sorted[:, h, t, :].rearrange("p (b i o) -> p b o i", i=4, o=C_CH),
-                        in_=g_raw[:, :, t, :, h].rearrange("p o (b i) -> p b o i", i=4),
+                        out=g_sorted[:, h - 1, t, :].rearrange("p (b i o) -> p b o i", i=4, o=C_CH),
+                        in_=g_raw_of[g][:, :, t, :, h - 1].rearrange("p o (b i) -> p b o i", i=4),
                     )
-            return g_sorted
+            g_sorted_of[g] = g_sorted
 
-        def hits(z, g_sorted):
-            z1 = z[1][:].rearrange("p q t k -> p q (t k)")
-            z2 = z[2][:].rearrange("p q t k -> p q (t k)")
-            z3 = z[3][:].rearrange("p q t k -> p (q t k)")
-            g3 = g_sorted[:, 2].rearrange("p t k -> p (t k)")
-            dz_a = work.tile([P, 4, GT, K], BF16)
-            dz_b = work.tile([P, 2, GT, K], BF16)
+        def hits(g):
+            gt = GROUP_TILES[g]
+            z1 = z_of[g][1][:].rearrange("p q t k -> p q (t k)")
+            z2 = z_of[g][2][:].rearrange("p q t k -> p q (t k)")
+            dz_a = work.tile([P, 4, gt, K], BF16, name="dz_a")
+            dz_b = work.tile([P, 2, gt, K], BF16, name="dz_b")
             a_planes = dz_a[:].rearrange("p q t k -> p q (t k)")
             b_planes = dz_b[:].rearrange("p q t k -> p q (t k)")
-
-            top = work.tile([P, GC], F32)
+            top = work.tile([P, gt * K], F32, name="top")
             nc.vector.scalar_tensor_tensor(
                 out=top[:], in0=z1[:, 0], scalar=SMALLEST_NORMAL, in1=z1[:, 1],
                 op0=ALU.max, op1=ALU.max,
@@ -139,22 +150,15 @@ def tile_vrtconv_t_v_kernel(
             )
             nc.vector.tensor_tensor(
                 out=a_planes[:, 0:3], in0=z1,
-                in1=top[:].unsqueeze(1).to_broadcast([P, 3, GC]), op=ALU.is_ge,
+                in1=top[:].unsqueeze(1).to_broadcast([P, 3, gt * K]), op=ALU.is_ge,
             )
-            nc.vector.scalar_tensor_tensor(
-                out=a_planes[:, 3], in0=z3, scalar=0.0, in1=g3, op0=ALU.is_gt, op1=ALU.mult,
-            )
-            return dz_a, dz_b
+            dz_of[g] = (dz_a, dz_b)
 
-        def share_and_mask(dz_a, dz_b, g_sorted):
-            a_planes = dz_a[:].rearrange("p q t k -> p q (t k)")
-            b_planes = dz_b[:].rearrange("p q t k -> p q (t k)")
-            g1 = g_sorted[:, 0].rearrange("p t k -> p (t k)")
-            g2 = g_sorted[:, 1].rearrange("p t k -> p (t k)")
-
-            share1 = work.tile([P, GT, K], BF16)
-            for t in range(GT):
-                count = cnt_pool.tile([P, K], F32)
+        def count_hits(g):
+            dz_a = dz_of[g][0]
+            share1 = work.tile([P, GROUP_TILES[g], K], BF16, name="share1")
+            for t in range(GROUP_TILES[g]):
+                count = cnt_pool.tile([P, K], F32, name="count")
                 for q in range(3):
                     nc.tensor.matmul(
                         out=count[:], lhsT=ident_bf16[:], rhs=dz_a[:, q, t, :],
@@ -163,96 +167,146 @@ def tile_vrtconv_t_v_kernel(
                 nc.scalar.activation(
                     out=share1[:, t, :], in_=count[:], func=ACT.Copy, scale=-0.5, bias=1.5
                 )
-            share2 = work.tile([P, GC], BF16)
+            share1_of[g] = share1
+
+        def early_products(g):
+            gt = GROUP_TILES[g]
+            dz_a, dz_b = dz_of[g]
+            a_planes = dz_a[:].rearrange("p q t k -> p q (t k)")
+            b_planes = dz_b[:].rearrange("p q t k -> p q (t k)")
+            grad = g_sorted_of[g][:].rearrange("p h t k -> p h (t k)")
+            z3 = z_of[g][3][:].rearrange("p q t k -> p (q t k)")
+            share2 = work.tile([P, gt * K], BF16, name="share2")
             nc.vector.tensor_tensor(
                 out=share2[:], in0=b_planes[:, 0], in1=b_planes[:, 1], op=ALU.add
+            )
+            nc.vector.scalar_tensor_tensor(
+                out=a_planes[:, 3], in0=z3, scalar=0.0, in1=grad[:, 2], op0=ALU.is_gt, op1=ALU.mult,
             )
             nc.vector.tensor_scalar(
                 out=share2[:], in0=share2[:], scalar1=-0.5, scalar2=1.5, op0=ALU.mult, op1=ALU.add
             )
-            nc.vector.tensor_tensor(out=share2[:], in0=share2[:], in1=g2, op=ALU.mult)
-            flat1 = share1[:].rearrange("p t k -> p (t k)")
+            share2_of[g] = share2
+
+        def late_products(g):
+            gt = GROUP_TILES[g]
+            dz_a, dz_b = dz_of[g]
+            a_planes = dz_a[:].rearrange("p q t k -> p q (t k)")
+            b_planes = dz_b[:].rearrange("p q t k -> p q (t k)")
+            grad = g_sorted_of[g][:].rearrange("p h t k -> p h (t k)")
+            share1 = share1_of[g][:].rearrange("p t k -> p (t k)")
+            share2 = share2_of[g]
+            nc.vector.tensor_tensor(out=share2[:], in0=share2[:], in1=grad[:, 1], op=ALU.mult)
             nc.vector.scalar_tensor_tensor(
-                out=flat1, in0=flat1, scalar=1.0 / 3.0, in1=g1, op0=ALU.max, op1=ALU.mult
+                out=share1, in0=share1, scalar=1.0 / 3.0, in1=grad[:, 0], op0=ALU.max, op1=ALU.mult
             )
             nc.vector.tensor_tensor(
                 out=b_planes, in0=b_planes,
-                in1=share2[:].unsqueeze(1).to_broadcast([P, 2, GC]), op=ALU.mult,
+                in1=share2[:].unsqueeze(1).to_broadcast([P, 2, gt * K]), op=ALU.mult,
             )
             nc.vector.tensor_tensor(
                 out=a_planes[:, 0:3], in0=a_planes[:, 0:3],
-                in1=flat1.unsqueeze(1).to_broadcast([P, 3, GC]), op=ALU.mult,
+                in1=share1.unsqueeze(1).to_broadcast([P, 3, gt * K]), op=ALU.mult,
             )
 
-        def transpose_and_quantise(dz, planes, label):
-            slots = GT * planes
-            grouped = work.tile([P, slots, P, 4], BF16, align_bytes=64, name="grouped" + label)
-            grouped_words = grouped[:].bitcast(F32)
-            for pair in range(slots // 2):
-                xt = xt_pool.tile([P, 2, 2, P], F32)
-                for i in range(2):
-                    t, q = divmod(2 * pair + i, planes)
-                    words = dz[:, q, t, :].bitcast(F32)
-                    for u in range(2):
-                        nc.tensor.transpose(
-                            out=xt[:, i, u, :], in_=words[:, u * P : (u + 1) * P],
-                            identity=ident_f32[:],
-                        )
-                nc.scalar.copy(
-                    out=grouped_words[:, 2 * pair : 2 * pair + 2],
-                    in_=xt[:].rearrange("p i u s -> p i s u"),
-                )
-            codes = work.tile([P, slots, P], U32, align_bytes=64, name="codes" + label)
-            scales = work.tile([P, slots, P], U8, align_bytes=64, name="scales" + label)
-            nc.vector.quantize_mx(
-                out=codes[:].rearrange("p n s -> p (n s)").bitcast(E5M2_X4),
-                scales=scales[:].rearrange("p n s -> p (n s)"),
-                in_=grouped[:].rearrange("p n s t -> p (n s t)"),
-            )
-            return codes, scales
-
-        def multiply_and_store(g, quantised_a, quantised_b):
-            staged = work.tile([P, C_CH, GT, L, D], F32)
-            for t in range(GT):
-                acc = [acc_pool.tile([P, N_COLS], F32, name="acc%d" % l) for l in range(L)]
-                for h in (1, 2, 3):
-                    for p in range(L - h + 1):
-                        if h == 2:
-                            (codes, scales), slot = quantised_b, t * 2 + p
-                        else:
-                            (codes, scales), slot = quantised_a, t * 4 + (p if h == 1 else 3)
-                        for a in range(h):
-                            w_slot = first_weight_slot(h) + a
-                            nc.tensor.matmul_mx(
-                                out=acc[p + a][:],
-                                lhsT=codes[:, slot, :].bitcast(E5M2_X4),
-                                lhsT_scale=scales[:, slot, :],
-                                rhs=w_codes[:, w_slot, :].bitcast(E4M3_X4),
-                                rhs_scale=w_scales[:, w_slot, :],
-                                start=(h == 1),
-                                stop=(h == 3),
+        def transpose(g):
+            grouped_of[g] = {}
+            dz_a, dz_b = dz_of[g]
+            for dz, planes, label in ((dz_b, 2, "B"), (dz_a, 4, "A")):
+                slots = GROUP_TILES[g] * planes
+                grouped = work.tile([P, slots, P, 4], BF16, align_bytes=64, name="grouped" + label)
+                grouped_words = grouped[:].bitcast(F32)
+                for pair in range(slots // 2):
+                    xt = xt_pool.tile([P, 2, 2, P], F32, name="xt")
+                    for i in range(2):
+                        t, q = divmod(2 * pair + i, planes)
+                        words = dz[:, q, t, :].bitcast(F32)
+                        for u in range(2):
+                            nc.tensor.transpose(
+                                out=xt[:, i, u, :], in_=words[:, u * P : (u + 1) * P],
+                                identity=ident_f32[:],
                             )
-                for l in range(L):
                     nc.scalar.copy(
+                        out=grouped_words[:, 2 * pair : 2 * pair + 2],
+                        in_=xt[:].rearrange("p i u s -> p i s u"),
+                    )
+                grouped_of[g][label] = grouped
+
+        def quantise(g):
+            quantised_of[g] = {}
+            for label in ("B", "A"):
+                grouped = grouped_of[g][label]
+                slots = grouped.shape[1]
+                codes = work.tile([P, slots, P], U32, align_bytes=64, name="codes" + label)
+                scales = work.tile([P, slots, P], U8, align_bytes=64, name="scales" + label)
+                nc.vector.quantize_mx(
+                    out=codes[:].rearrange("p n s -> p (n s)").bitcast(E5M2_X4),
+                    scales=scales[:].rearrange("p n s -> p (n s)"),
+                    in_=grouped[:].rearrange("p n s t -> p (n s t)"),
+                )
+                quantised_of[g][label] = (codes, scales)
+
+        def multiply_and_store(g):
+            gt = GROUP_TILES[g]
+            first_pass_of_row = {p + a: i for i, (h, p, a) in reversed(list(enumerate(PASSES)))}
+            staged = work.tile([P, C_CH, gt, L, D], F32, name="staged")
+            for t in range(gt):
+                acc = [acc_pool.tile([P, N_COLS], F32, name="acc%d" % l) for l in range(L)]
+                for i, (h, p, a) in enumerate(PASSES):
+                    if h == 2:
+                        (codes, scales), slot = quantised_of[g]["B"], t * 2 + p
+                    else:
+                        (codes, scales), slot = quantised_of[g]["A"], t * 4 + (p if h == 1 else 3)
+                    w_slot = first_weight_slot(h) + a
+                    nc.tensor.matmul_mx(
+                        out=acc[p + a][:],
+                        lhsT=codes[:, slot, :].bitcast(E5M2_X4),
+                        lhsT_scale=scales[:, slot, :],
+                        rhs=w_codes[:, w_slot, :].bitcast(E4M3_X4),
+                        rhs_scale=w_scales[:, w_slot, :],
+                        start=(i == first_pass_of_row[p + a]),
+                        stop=(h == 3),
+                    )
+                for l in range(L):
+                    copy_out = nc.vector.tensor_copy if (g == GROUPS - 1 and l == 1) else nc.scalar.copy
+                    copy_out(
                         out=staged[:, :, t, l, :],
                         in_=acc[l][:].rearrange("p (c d) -> p c d", d=D),
                     )
-            nc.sync.dma_start(
-                out=out_view[:, :, g * GT : (g + 1) * GT, :],
+            nc.scalar.dma_start(
+                out=out_view[:, :, tiles_of(g), :],
                 in_=staged[:].rearrange("p c t l d -> p c t (l d)"),
             )
 
-        loaded = load_group(0)
-        w_raw = load_weights()
+        load_group(0)
+        load_weight(1)
+        load_weight(2)
+        load_group(1)
+        load_weight(3)
+        sort_grad(0)
         for g in range(GROUPS):
-            z, g_raw = loaded
-            if g + 1 < GROUPS:
-                loaded = load_group(g + 1)
-            g_sorted = sort_grad(g_raw)
-            dz_a, dz_b = hits(z, g_sorted)
-            share_and_mask(dz_a, dz_b, g_sorted)
+            hits(g)
+            count_hits(g)
+            early_products(g)
+            if g == 1:
+                quantise_weights((1, 2))
+            if g == 2:
+                quantise_weights((3,))
+            if g >= 1:
+                quantise(g - 1)
             if g == 0:
-                quantise_weights(w_raw)
-            quantised_a = transpose_and_quantise(dz_a, 4, "A")
-            quantised_b = transpose_and_quantise(dz_b, 2, "B")
-            multiply_and_store(g, quantised_a, quantised_b)
+                regroup_weights((1, 2))
+            if g == 1:
+                regroup_weights((3,))
+            if g + 1 < GROUPS:
+                sort_grad(g + 1)
+            if g == 2:
+                multiply_and_store(0)
+            if g >= 2:
+                multiply_and_store(g - 1)
+            late_products(g)
+            if g + 2 < GROUPS:
+                load_group(g + 2)
+            transpose(g)
+        quantise(GROUPS - 1)
+        multiply_and_store(GROUPS - 1)

@@ -77,6 +77,7 @@ def tile_vrtconv_t_v_kernel(
         z_of, g_raw_of, g_sorted_of, dz_of, share1_of, share2_of, grouped_of, quantised_of = (
             {}, {}, {}, {}, {}, {}, {}, {},
         )
+        staged_of = {}
 
         def load_group(g):
             gt = GROUP_TILES[g]
@@ -246,37 +247,39 @@ def tile_vrtconv_t_v_kernel(
                 )
                 quantised_of[g][label] = (codes, scales)
 
-        def multiply_and_store(g):
+        def multiply_tile(g, t):
             gt = GROUP_TILES[g]
             first_pass_of_row = {p + a: i for i, (h, p, a) in reversed(list(enumerate(PASSES)))}
-            staged = work.tile([P, C_CH, gt, L, D], F32, name="staged")
-            for t in range(gt):
-                acc = [acc_pool.tile([P, N_COLS], F32, name="acc%d" % l) for l in range(L)]
-                for i, (h, p, a) in enumerate(PASSES):
-                    if h == 2:
-                        (codes, scales), slot = quantised_of[g]["B"], t * 2 + p
-                    else:
-                        (codes, scales), slot = quantised_of[g]["A"], t * 4 + (p if h == 1 else 3)
-                    w_slot = first_weight_slot(h) + a
-                    nc.tensor.matmul_mx(
-                        out=acc[p + a][:],
-                        lhsT=codes[:, slot, :].bitcast(E5M2_X4),
-                        lhsT_scale=scales[:, slot, :],
-                        rhs=w_codes[:, w_slot, :].bitcast(E4M3_X4),
-                        rhs_scale=w_scales[:, w_slot, :],
-                        start=(i == first_pass_of_row[p + a]),
-                        stop=(h == 3),
-                    )
-                for l in range(L):
-                    copy_out = nc.vector.tensor_copy if (g == GROUPS - 1 and l == 1) else nc.scalar.copy
-                    copy_out(
-                        out=staged[:, :, t, l, :],
-                        in_=acc[l][:].rearrange("p (c d) -> p c d", d=D),
-                    )
-            nc.scalar.dma_start(
-                out=out_view[:, :, tiles_of(g), :],
-                in_=staged[:].rearrange("p c t l d -> p c t (l d)"),
-            )
+            if t == 0:
+                staged_of[g] = work.tile([P, C_CH, gt, L, D], F32, name="staged")
+            staged = staged_of[g]
+            acc = [acc_pool.tile([P, N_COLS], F32, name="acc%d" % l) for l in range(L)]
+            for i, (h, p, a) in enumerate(PASSES):
+                if h == 2:
+                    (codes, scales), slot = quantised_of[g]["B"], t * 2 + p
+                else:
+                    (codes, scales), slot = quantised_of[g]["A"], t * 4 + (p if h == 1 else 3)
+                w_slot = first_weight_slot(h) + a
+                nc.tensor.matmul_mx(
+                    out=acc[p + a][:],
+                    lhsT=codes[:, slot, :].bitcast(E5M2_X4),
+                    lhsT_scale=scales[:, slot, :],
+                    rhs=w_codes[:, w_slot, :].bitcast(E4M3_X4),
+                    rhs_scale=w_scales[:, w_slot, :],
+                    start=(i == first_pass_of_row[p + a]),
+                    stop=(h == 3),
+                )
+            for l in range(L):
+                copy_out = nc.vector.tensor_copy if (g == GROUPS - 1 and l == 1) else nc.scalar.copy
+                copy_out(
+                    out=staged[:, :, t, l, :],
+                    in_=acc[l][:].rearrange("p (c d) -> p c d", d=D),
+                )
+            if t == gt - 1:
+                nc.scalar.dma_start(
+                    out=out_view[:, :, tiles_of(g), :],
+                    in_=staged[:].rearrange("p c t l d -> p c t (l d)"),
+                )
 
         load_group(0)
         load_weight(1)
@@ -284,6 +287,7 @@ def tile_vrtconv_t_v_kernel(
         load_group(1)
         load_weight(3)
         sort_grad(0)
+        due = []
         for g in range(GROUPS):
             hits(g)
             count_hits(g)
@@ -294,19 +298,23 @@ def tile_vrtconv_t_v_kernel(
                 quantise_weights((3,))
             if g >= 1:
                 quantise(g - 1)
+                due.extend([(g - 1, t) for t in range(GROUP_TILES[g - 1])])
             if g == 0:
                 regroup_weights((1, 2))
             if g == 1:
                 regroup_weights((3,))
             if g + 1 < GROUPS:
                 sort_grad(g + 1)
-            if g == 2:
-                multiply_and_store(0)
             if g >= 2:
-                multiply_and_store(g - 1)
+                multiply_tile(*due[0])
             late_products(g)
             if g + 2 < GROUPS:
                 load_group(g + 2)
             transpose(g)
+            if g >= 2:
+                for group_and_tile in due[1:]:
+                    multiply_tile(*group_and_tile)
+                due = []
         quantise(GROUPS - 1)
-        multiply_and_store(GROUPS - 1)
+        for t in range(GROUP_TILES[GROUPS - 1]):
+            multiply_tile(GROUPS - 1, t)

@@ -21,18 +21,30 @@ J = 32
 K = J * C_CH
 N_COLS = C_CH * D
 TILES = S // P
-GROUP_TILES = (1, 1, 2, 2, 1, 1)
-GROUPS = len(GROUP_TILES)
 SMALLEST_NORMAL = 2.0**-126
-PASSES = [(h, p, a) for h in (2, 1, 3) for p in range(L - h + 1) for a in range(h)]
 
-FLOPS = 2 * K * S * N_COLS * len(PASSES)
-BYTES = 4 * 6 * S * K + 2 * C_CH * S * 96 + 2 * K * N_COLS * 6 + 4 * C_CH * S * L * D
-
+SINGLE_TILE_GROUPS_AT_EACH_END = 2
+GROUP_TILES = (
+    (1,) * SINGLE_TILE_GROUPS_AT_EACH_END
+    + (2,) * ((TILES - 2 * SINGLE_TILE_GROUPS_AT_EACH_END) // 2)
+    + (1,) * SINGLE_TILE_GROUPS_AT_EACH_END
+)
+GROUPS = len(GROUP_TILES)
 assert sum(GROUP_TILES) == TILES
 
+WEIGHT_BATCHES = ((1, 2), (3,))
+BLOCKS_IN_A_BATCH = 3
+WEIGHT_BLOCKS = 6
 
-def first_weight_slot(h):
+PASSES = [(2, p, a) for p in range(2) for a in range(2)] + [
+    one_pass for l in range(L) for one_pass in ((1, l, 0), (3, 0, l))
+]
+
+FLOPS = 2 * K * S * N_COLS * len(PASSES)
+BYTES = 4 * 6 * S * K + 2 * C_CH * S * L * J + 2 * K * N_COLS * WEIGHT_BLOCKS + 4 * C_CH * S * L * D
+
+
+def first_weight_block(h):
     return h * (h - 1) // 2
 
 
@@ -56,7 +68,7 @@ def tile_vrtconv_t_v_kernel(
 
     with ExitStack() as stack:
         keep = stack.enter_context(tc.tile_pool(name="keep", bufs=1))
-        wstage = stack.enter_context(tc.tile_pool(name="wstage", bufs=3))
+        wstage = stack.enter_context(tc.tile_pool(name="wstage", bufs=BLOCKS_IN_A_BATCH))
         loads = stack.enter_context(tc.tile_pool(name="loads", bufs=2))
         work = stack.enter_context(tc.tile_pool(name="work", bufs=2))
         acc_pool = stack.enter_context(tc.psum_pool(name="acc", bufs=1))
@@ -71,20 +83,19 @@ def tile_vrtconv_t_v_kernel(
 
         w_raw = {}
         w_grouped = {}
-        w_codes = keep.tile([P, 6, N_COLS], U32, align_bytes=64)
-        w_scales = keep.tile([P, 6, N_COLS], U8, align_bytes=64)
+        w_codes = keep.tile([P, WEIGHT_BLOCKS, N_COLS], U32, align_bytes=64)
+        w_scales = keep.tile([P, WEIGHT_BLOCKS, N_COLS], U8, align_bytes=64)
 
-        z_of, g_raw_of, g_sorted_of, dz_of, share1_of, share2_of, grouped_of, quantised_of = (
-            {}, {}, {}, {}, {}, {}, {}, {},
-        )
-        staged_of = {}
+        z_of, g_raw_of, g_sorted_of, dz_of, share1_of, share2_of = {}, {}, {}, {}, {}, {}
+        grouped_of, quantised_of, staged_of = {}, {}, {}
 
         def load_group(g):
             gt = GROUP_TILES[g]
             z = {h: loads.tile([P, L - h + 1, gt, K], F32, name="z%d" % h) for h in (1, 2, 3)}
             g_raw = loads.tile([P, C_CH, gt, J, L], BF16, name="g_raw")
-            for h in (1, 2):
-                nc.sync.dma_start(out=z[h][:], in_=conv_views[h][:, :, tiles_of(g), :])
+            nc.sync.dma_start(out=z[1][:, 0:2], in_=conv_views[1][:, 0:2, tiles_of(g), :])
+            nc.sync.dma_start(out=z[2][:], in_=conv_views[2][:, :, tiles_of(g), :])
+            nc.sync.dma_start(out=z[1][:, 2:3], in_=conv_views[1][:, 2:3, tiles_of(g), :])
             nc.sync.dma_start(
                 out=g_raw[:].rearrange("p o t j h -> p o t (j h)"),
                 in_=grad_view[:, :, tiles_of(g), :],
@@ -102,19 +113,19 @@ def tile_vrtconv_t_v_kernel(
 
         def regroup_weights(heights):
             for h in heights:
-                by_row = w_raw[h][:].rearrange("p t (c a d) -> p a c d t", a=h, d=D)
+                by_kernel_row = w_raw[h][:].rearrange("p t (c a d) -> p a c d t", a=h, d=D)
                 for a in range(h):
                     grouped = wstage.tile([P, C_CH, D, 4], BF16, align_bytes=64, name="w_grouped")
-                    nc.scalar.copy(out=grouped[:], in_=by_row[:, a])
-                    w_grouped[first_weight_slot(h) + a] = grouped
+                    nc.scalar.copy(out=grouped[:], in_=by_kernel_row[:, a])
+                    w_grouped[first_weight_block(h) + a] = grouped
 
         def quantise_weights(heights):
             for h in heights:
-                for slot in range(first_weight_slot(h), first_weight_slot(h) + h):
+                for block in range(first_weight_block(h), first_weight_block(h) + h):
                     nc.vector.quantize_mx(
-                        out=w_codes[:, slot, :].bitcast(E4M3_X4),
-                        scales=w_scales[:, slot, :],
-                        in_=w_grouped[slot][:].rearrange("p c d t -> p (c d t)"),
+                        out=w_codes[:, block, :].bitcast(E4M3_X4),
+                        scales=w_scales[:, block, :],
+                        in_=w_grouped[block][:].rearrange("p c d t -> p (c d t)"),
                     )
 
         def sort_grad(g):
@@ -131,58 +142,57 @@ def tile_vrtconv_t_v_kernel(
             gt = GROUP_TILES[g]
             z1 = z_of[g][1][:].rearrange("p q t k -> p q (t k)")
             z2 = z_of[g][2][:].rearrange("p q t k -> p q (t k)")
-            dz_a = work.tile([P, 4, gt, K], BF16, name="dz_a")
-            dz_b = work.tile([P, 2, gt, K], BF16, name="dz_b")
-            a_planes = dz_a[:].rearrange("p q t k -> p q (t k)")
-            b_planes = dz_b[:].rearrange("p q t k -> p q (t k)")
+            dz_13 = work.tile([P, 4, gt, K], BF16, name="dz_13")
+            dz_2 = work.tile([P, 2, gt, K], BF16, name="dz_2")
+            planes_13 = dz_13[:].rearrange("p q t k -> p q (t k)")
+            planes_2 = dz_2[:].rearrange("p q t k -> p q (t k)")
             top = work.tile([P, gt * K], F32, name="top")
             nc.vector.scalar_tensor_tensor(
                 out=top[:], in0=z1[:, 0], scalar=SMALLEST_NORMAL, in1=z1[:, 1],
                 op0=ALU.max, op1=ALU.max,
             )
             nc.vector.scalar_tensor_tensor(
-                out=b_planes[:, 0], in0=z2[:, 1], scalar=SMALLEST_NORMAL, in1=z2[:, 0],
+                out=planes_2[:, 0], in0=z2[:, 1], scalar=SMALLEST_NORMAL, in1=z2[:, 0],
                 op0=ALU.max, op1=ALU.is_le,
             )
             nc.vector.tensor_tensor(out=top[:], in0=top[:], in1=z1[:, 2], op=ALU.max)
             nc.vector.scalar_tensor_tensor(
-                out=b_planes[:, 1], in0=z2[:, 0], scalar=SMALLEST_NORMAL, in1=z2[:, 1],
+                out=planes_2[:, 1], in0=z2[:, 0], scalar=SMALLEST_NORMAL, in1=z2[:, 1],
                 op0=ALU.max, op1=ALU.is_le,
             )
             nc.vector.tensor_tensor(
-                out=a_planes[:, 0:3], in0=z1,
+                out=planes_13[:, 0:3], in0=z1,
                 in1=top[:].unsqueeze(1).to_broadcast([P, 3, gt * K]), op=ALU.is_ge,
             )
-            dz_of[g] = (dz_a, dz_b)
+            dz_of[g] = (dz_13, dz_2)
 
         def count_hits(g):
-            dz_a = dz_of[g][0]
-            share1 = work.tile([P, GROUP_TILES[g], K], BF16, name="share1")
-            for t in range(GROUP_TILES[g]):
-                count = cnt_pool.tile([P, K], F32, name="count")
+            gt = GROUP_TILES[g]
+            dz_13 = dz_of[g][0]
+            count = cnt_pool.tile([P, gt, K], BF16, name="count")
+            for t in range(gt):
                 for q in range(3):
                     nc.tensor.matmul(
-                        out=count[:], lhsT=ident_bf16[:], rhs=dz_a[:, q, t, :],
+                        out=count[:, t, :], lhsT=ident_bf16[:], rhs=dz_13[:, q, t, :],
                         start=(q == 0), stop=(q == 2),
                     )
-                nc.scalar.activation(
-                    out=share1[:, t, :], in_=count[:], func=ACT.Copy, scale=-0.5, bias=1.5
-                )
+            share1 = work.tile([P, gt, K], BF16, name="share1")
+            nc.scalar.activation(out=share1[:], in_=count[:], func=ACT.Copy, scale=-0.5, bias=1.5)
             share1_of[g] = share1
 
         def early_products(g):
             gt = GROUP_TILES[g]
-            dz_a, dz_b = dz_of[g]
-            a_planes = dz_a[:].rearrange("p q t k -> p q (t k)")
-            b_planes = dz_b[:].rearrange("p q t k -> p q (t k)")
+            dz_13, dz_2 = dz_of[g]
+            planes_13 = dz_13[:].rearrange("p q t k -> p q (t k)")
+            planes_2 = dz_2[:].rearrange("p q t k -> p q (t k)")
             grad = g_sorted_of[g][:].rearrange("p h t k -> p h (t k)")
             z3 = z_of[g][3][:].rearrange("p q t k -> p (q t k)")
             share2 = work.tile([P, gt * K], BF16, name="share2")
             nc.vector.tensor_tensor(
-                out=share2[:], in0=b_planes[:, 0], in1=b_planes[:, 1], op=ALU.add
+                out=share2[:], in0=planes_2[:, 0], in1=planes_2[:, 1], op=ALU.add
             )
             nc.vector.scalar_tensor_tensor(
-                out=a_planes[:, 3], in0=z3, scalar=0.0, in1=grad[:, 2], op0=ALU.is_gt, op1=ALU.mult,
+                out=planes_13[:, 3], in0=z3, scalar=0.0, in1=grad[:, 2], op0=ALU.is_gt, op1=ALU.mult,
             )
             nc.vector.tensor_scalar(
                 out=share2[:], in0=share2[:], scalar1=-0.5, scalar2=1.5, op0=ALU.mult, op1=ALU.add
@@ -191,9 +201,9 @@ def tile_vrtconv_t_v_kernel(
 
         def late_products(g):
             gt = GROUP_TILES[g]
-            dz_a, dz_b = dz_of[g]
-            a_planes = dz_a[:].rearrange("p q t k -> p q (t k)")
-            b_planes = dz_b[:].rearrange("p q t k -> p q (t k)")
+            dz_13, dz_2 = dz_of[g]
+            planes_13 = dz_13[:].rearrange("p q t k -> p q (t k)")
+            planes_2 = dz_2[:].rearrange("p q t k -> p q (t k)")
             grad = g_sorted_of[g][:].rearrange("p h t k -> p h (t k)")
             share1 = share1_of[g][:].rearrange("p t k -> p (t k)")
             share2 = share2_of[g]
@@ -202,20 +212,20 @@ def tile_vrtconv_t_v_kernel(
                 out=share1, in0=share1, scalar=1.0 / 3.0, in1=grad[:, 0], op0=ALU.max, op1=ALU.mult
             )
             nc.vector.tensor_tensor(
-                out=b_planes, in0=b_planes,
+                out=planes_2, in0=planes_2,
                 in1=share2[:].unsqueeze(1).to_broadcast([P, 2, gt * K]), op=ALU.mult,
             )
             nc.vector.tensor_tensor(
-                out=a_planes[:, 0:3], in0=a_planes[:, 0:3],
+                out=planes_13[:, 0:3], in0=planes_13[:, 0:3],
                 in1=share1.unsqueeze(1).to_broadcast([P, 3, gt * K]), op=ALU.mult,
             )
 
         def transpose(g):
             grouped_of[g] = {}
-            dz_a, dz_b = dz_of[g]
-            for dz, planes, label in ((dz_b, 2, "B"), (dz_a, 4, "A")):
+            dz_13, dz_2 = dz_of[g]
+            for dz, planes, label in ((dz_2, 2, "2"), (dz_13, 4, "13")):
                 slots = GROUP_TILES[g] * planes
-                grouped = work.tile([P, slots, P, 4], BF16, align_bytes=64, name="grouped" + label)
+                grouped = work.tile([P, slots, P, 4], BF16, align_bytes=64, name="grouped_" + label)
                 grouped_words = grouped[:].bitcast(F32)
                 for pair in range(slots // 2):
                     xt = xt_pool.tile([P, 2, 2, P], F32, name="xt")
@@ -235,11 +245,11 @@ def tile_vrtconv_t_v_kernel(
 
         def quantise(g):
             quantised_of[g] = {}
-            for label in ("B", "A"):
+            for label in ("2", "13"):
                 grouped = grouped_of[g][label]
                 slots = grouped.shape[1]
-                codes = work.tile([P, slots, P], U32, align_bytes=64, name="codes" + label)
-                scales = work.tile([P, slots, P], U8, align_bytes=64, name="scales" + label)
+                codes = work.tile([P, slots, P], U32, align_bytes=64, name="codes_" + label)
+                scales = work.tile([P, slots, P], U8, align_bytes=64, name="scales_" + label)
                 nc.vector.quantize_mx(
                     out=codes[:].rearrange("p n s -> p (n s)").bitcast(E5M2_X4),
                     scales=scales[:].rearrange("p n s -> p (n s)"),
@@ -256,16 +266,16 @@ def tile_vrtconv_t_v_kernel(
             acc = [acc_pool.tile([P, N_COLS], F32, name="acc%d" % l) for l in range(L)]
             for i, (h, p, a) in enumerate(PASSES):
                 if h == 2:
-                    (codes, scales), slot = quantised_of[g]["B"], t * 2 + p
+                    (codes, scales), slot = quantised_of[g]["2"], t * 2 + p
                 else:
-                    (codes, scales), slot = quantised_of[g]["A"], t * 4 + (p if h == 1 else 3)
-                w_slot = first_weight_slot(h) + a
+                    (codes, scales), slot = quantised_of[g]["13"], t * 4 + (p if h == 1 else 3)
+                block = first_weight_block(h) + a
                 nc.tensor.matmul_mx(
                     out=acc[p + a][:],
                     lhsT=codes[:, slot, :].bitcast(E5M2_X4),
                     lhsT_scale=scales[:, slot, :],
-                    rhs=w_codes[:, w_slot, :].bitcast(E4M3_X4),
-                    rhs_scale=w_scales[:, w_slot, :],
+                    rhs=w_codes[:, block, :].bitcast(E4M3_X4),
+                    rhs_scale=w_scales[:, block, :],
                     start=(i == first_pass_of_row[p + a]),
                     stop=(h == 3),
                 )
@@ -281,37 +291,34 @@ def tile_vrtconv_t_v_kernel(
                     in_=staged[:].rearrange("p c t l d -> p c t (l d)"),
                 )
 
-        load_group(0)
-        load_weight(1)
-        load_weight(2)
-        load_group(1)
-        load_weight(3)
+        for g, batch in enumerate(WEIGHT_BATCHES):
+            load_group(g)
+            for h in batch:
+                load_weight(h)
         sort_grad(0)
+
+        first_turn_of_products = len(WEIGHT_BATCHES)
         due = []
         for g in range(GROUPS):
             hits(g)
             count_hits(g)
             early_products(g)
-            if g == 1:
-                quantise_weights((1, 2))
-            if g == 2:
-                quantise_weights((3,))
+            if 1 <= g <= len(WEIGHT_BATCHES):
+                quantise_weights(WEIGHT_BATCHES[g - 1])
             if g >= 1:
                 quantise(g - 1)
                 due.extend([(g - 1, t) for t in range(GROUP_TILES[g - 1])])
-            if g == 0:
-                regroup_weights((1, 2))
-            if g == 1:
-                regroup_weights((3,))
+            if g < len(WEIGHT_BATCHES):
+                regroup_weights(WEIGHT_BATCHES[g])
             if g + 1 < GROUPS:
                 sort_grad(g + 1)
-            if g >= 2:
+            if g >= first_turn_of_products:
                 multiply_tile(*due[0])
             late_products(g)
             if g + 2 < GROUPS:
                 load_group(g + 2)
             transpose(g)
-            if g >= 2:
+            if g >= first_turn_of_products:
                 for group_and_tile in due[1:]:
                     multiply_tile(*group_and_tile)
                 due = []

@@ -32,6 +32,10 @@ GROUP_TILES = (
 GROUPS = len(GROUP_TILES)
 assert sum(GROUP_TILES) == TILES
 
+LOAD_BUFS = 3
+GRAD_TILES = 2
+STORE_UNITS = ((0, 1), (2,), (3,), (4,), (5,))
+
 WEIGHT_BATCHES = ((1, 2), (3,))
 BLOCKS_IN_A_BATCH = 3
 WEIGHT_BLOCKS = 6
@@ -69,7 +73,8 @@ def tile_vrtconv_t_v_kernel(
     with ExitStack() as stack:
         keep = stack.enter_context(tc.tile_pool(name="keep", bufs=1))
         wstage = stack.enter_context(tc.tile_pool(name="wstage", bufs=BLOCKS_IN_A_BATCH))
-        loads = stack.enter_context(tc.tile_pool(name="loads", bufs=2))
+        loads = stack.enter_context(tc.tile_pool(name="loads", bufs=LOAD_BUFS))
+        big = stack.enter_context(tc.tile_pool(name="big", bufs=2))
         work = stack.enter_context(tc.tile_pool(name="work", bufs=2))
         acc_pool = stack.enter_context(tc.psum_pool(name="acc", bufs=1))
         xt_pool = stack.enter_context(tc.psum_pool(name="xt", bufs=4))
@@ -82,38 +87,47 @@ def tile_vrtconv_t_v_kernel(
         make_identity(nc, ident_bf16[:])
 
         w_raw = {}
+        w_tile = [None]
+        g_unit_of = {}
         w_grouped = {}
         w_codes = keep.tile([P, WEIGHT_BLOCKS, N_COLS], U32, align_bytes=64)
         w_scales = keep.tile([P, WEIGHT_BLOCKS, N_COLS], U8, align_bytes=64)
 
-        z_of, g_raw_of, g_sorted_of, dz_of, share1_of, share2_of = {}, {}, {}, {}, {}, {}
+        z_of, g_sorted_of, dz_of, share1_of, share2_of = {}, {}, {}, {}, {}
         grouped_of, quantised_of, staged_of = {}, {}, {}
 
         def load_group(g):
             gt = GROUP_TILES[g]
             z = {h: loads.tile([P, L - h + 1, gt, K], F32, name="z%d" % h) for h in (1, 2, 3)}
-            g_raw = loads.tile([P, C_CH, gt, J, L], BF16, name="g_raw")
+            first = tiles_of(g).start
             nc.sync.dma_start(out=z[1][:, 0:2], in_=conv_views[1][:, 0:2, tiles_of(g), :])
             nc.sync.dma_start(out=z[2][:], in_=conv_views[2][:, :, tiles_of(g), :])
             nc.sync.dma_start(out=z[1][:, 2:3], in_=conv_views[1][:, 2:3, tiles_of(g), :])
-            nc.sync.dma_start(
-                out=g_raw[:].rearrange("p o t j h -> p o t (j h)"),
-                in_=grad_view[:, :, tiles_of(g), :],
-            )
+            if first % GRAD_TILES == 0:
+                g_raw = loads.tile([P, C_CH, GRAD_TILES, J, L], BF16, name="g_raw")
+                nc.sync.dma_start(
+                    out=g_raw[:].rearrange("p o t j h -> p o t (j h)"),
+                    in_=grad_view[:, :, first : first + GRAD_TILES, :],
+                )
+                g_unit_of[first // GRAD_TILES] = g_raw
             nc.sync.dma_start(out=z[3][:], in_=conv_views[3][:, :, tiles_of(g), :])
-            z_of[g], g_raw_of[g] = z, g_raw
+            z_of[g] = z
 
         def load_weight(h):
-            w_raw[h] = keep.tile([P, 4, h * N_COLS], BF16, name="w_raw%d" % h)
+            if h != 2:
+                w_tile[0] = big.tile([P, 4, 3 * N_COLS], BF16, name="big")
+            first_col = N_COLS if h == 2 else 0
+            w_raw[h] = w_tile[0][:, :, first_col : first_col + h * N_COLS]
             rows = weights[h].rearrange("j o c a d -> (j o) (c a d)")
-            nc.sync.dma_start(
-                out=w_raw[h][:].rearrange("p (u e) n -> p u (e n)", u=2),
-                in_=rows.rearrange("(u p e) n -> p u (e n)", u=2, e=2),
-            )
+            for u in range(2):
+                nc.sync.dma_start(
+                    out=w_raw[h][:, 2 * u : 2 * u + 2, :],
+                    in_=rows[u * 2 * P : (u + 1) * 2 * P, :].rearrange("(p e) n -> p e n", e=2),
+                )
 
         def regroup_weights(heights):
             for h in heights:
-                by_kernel_row = w_raw[h][:].rearrange("p t (c a d) -> p a c d t", a=h, d=D)
+                by_kernel_row = w_raw[h].rearrange("p t (c a d) -> p a c d t", a=h, d=D)
                 for a in range(h):
                     grouped = wstage.tile([P, C_CH, D, 4], BF16, align_bytes=64, name="w_grouped")
                     nc.scalar.copy(out=grouped[:], in_=by_kernel_row[:, a])
@@ -130,11 +144,13 @@ def tile_vrtconv_t_v_kernel(
 
         def sort_grad(g):
             g_sorted = work.tile([P, L, GROUP_TILES[g], K], BF16, name="g_sorted")
+            unit, offset = divmod(tiles_of(g).start, GRAD_TILES)
+            g_raw = g_unit_of[unit]
             for h in (3, 2, 1):
                 for t in range(GROUP_TILES[g]):
                     nc.scalar.copy(
                         out=g_sorted[:, h - 1, t, :].rearrange("p (b i o) -> p b o i", i=4, o=C_CH),
-                        in_=g_raw_of[g][:, :, t, :, h - 1].rearrange("p o (b i) -> p b o i", i=4),
+                        in_=g_raw[:, :, offset + t, :, h - 1].rearrange("p o (b i) -> p b o i", i=4),
                     )
             g_sorted_of[g] = g_sorted
 
@@ -260,9 +276,13 @@ def tile_vrtconv_t_v_kernel(
         def multiply_tile(g, t):
             gt = GROUP_TILES[g]
             first_pass_of_row = {p + a: i for i, (h, p, a) in reversed(list(enumerate(PASSES)))}
-            if t == 0:
-                staged_of[g] = work.tile([P, C_CH, gt, L, D], F32, name="staged")
-            staged = staged_of[g]
+            unit = [groups for groups in STORE_UNITS if g in groups][0]
+            unit_first = tiles_of(unit[0]).start
+            unit_tiles = tiles_of(unit[-1]).stop - unit_first
+            place = tiles_of(g).start + t - unit_first
+            if place == 0:
+                staged_of[unit] = big.tile([P, C_CH, unit_tiles, L, D], F32, name="big")
+            staged = staged_of[unit]
             acc = [acc_pool.tile([P, N_COLS], F32, name="acc%d" % l) for l in range(L)]
             for i, (h, p, a) in enumerate(PASSES):
                 if h == 2:
@@ -282,12 +302,12 @@ def tile_vrtconv_t_v_kernel(
             for l in range(L):
                 copy_out = nc.vector.tensor_copy if (g == GROUPS - 1 and l == 1) else nc.scalar.copy
                 copy_out(
-                    out=staged[:, :, t, l, :],
+                    out=staged[:, :, place, l, :],
                     in_=acc[l][:].rearrange("p (c d) -> p c d", d=D),
                 )
-            if t == gt - 1:
+            if place == unit_tiles - 1:
                 nc.scalar.dma_start(
-                    out=out_view[:, :, tiles_of(g), :],
+                    out=out_view[:, :, unit_first : unit_first + unit_tiles, :],
                     in_=staged[:].rearrange("p c t l d -> p c t (l d)"),
                 )
 
@@ -295,6 +315,8 @@ def tile_vrtconv_t_v_kernel(
             load_group(g)
             for h in batch:
                 load_weight(h)
+        for g in range(len(WEIGHT_BATCHES), LOAD_BUFS):
+            load_group(g)
         sort_grad(0)
 
         first_turn_of_products = len(WEIGHT_BATCHES)
@@ -315,8 +337,8 @@ def tile_vrtconv_t_v_kernel(
             if g >= first_turn_of_products:
                 multiply_tile(*due[0])
             late_products(g)
-            if g + 2 < GROUPS:
-                load_group(g + 2)
+            if g + LOAD_BUFS < GROUPS:
+                load_group(g + LOAD_BUFS)
             transpose(g)
             if g >= first_turn_of_products:
                 for group_and_tile in due[1:]:

@@ -85,6 +85,12 @@ def tile_vrtconv_t_v_kernel(
         make_identity(nc, ident_f32[:])
         ident_bf16 = keep.tile([P, P], BF16)
         make_identity(nc, ident_bf16[:])
+        minus_half = keep.tile([P, P], BF16)
+        nc.vector.tensor_scalar_mul(out=minus_half[:], in0=ident_bf16[:], scalar1=-0.5)
+        three_halves = keep.tile([P, P], BF16)
+        nc.vector.tensor_scalar_mul(out=three_halves[:], in0=ident_bf16[:], scalar1=1.5)
+        ones = keep.tile([P, K], BF16)
+        nc.vector.memset(ones[:], 1.0)
 
         w_raw = {}
         w_tile = [None]
@@ -94,7 +100,7 @@ def tile_vrtconv_t_v_kernel(
         w_scales = keep.tile([P, WEIGHT_BLOCKS, N_COLS], U8, align_bytes=64)
 
         z_of, g_sorted_of, dz_of, share1_of, share2_of = {}, {}, {}, {}, {}
-        grouped_of, quantised_of, staged_of = {}, {}, {}
+        grouped_of, quantised_of, staged_of, count_of = {}, {}, {}, {}
 
         def load_group(g):
             gt = GROUP_TILES[g]
@@ -146,11 +152,18 @@ def tile_vrtconv_t_v_kernel(
             g_sorted = work.tile([P, L, GROUP_TILES[g], K], BF16, name="g_sorted")
             unit, offset = divmod(tiles_of(g).start, GRAD_TILES)
             g_raw = g_unit_of[unit]
-            for h in (3, 2, 1):
-                for t in range(GROUP_TILES[g]):
+            if g > 0 and GROUP_TILES[g] == 1:
+                nc.scalar.copy(
+                    out=g_sorted[:, :, 0, :].rearrange("p h (b i o) -> p h b o i", i=4, o=C_CH),
+                    in_=g_raw[:, :, offset, :, :].rearrange("p o (b i) h -> p h b o i", i=4),
+                )
+            else:
+                for h in (3, 2, 1):
                     nc.scalar.copy(
-                        out=g_sorted[:, h - 1, t, :].rearrange("p (b i o) -> p b o i", i=4, o=C_CH),
-                        in_=g_raw[:, :, offset + t, :, h - 1].rearrange("p o (b i) -> p b o i", i=4),
+                        out=g_sorted[:, h - 1].rearrange("p t (b i o) -> p t b o i", i=4, o=C_CH),
+                        in_=g_raw[:, :, offset : offset + GROUP_TILES[g], :, h - 1].rearrange(
+                            "p o t (b i) -> p t b o i", i=4
+                        ),
                     )
             g_sorted_of[g] = g_sorted
 
@@ -187,14 +200,16 @@ def tile_vrtconv_t_v_kernel(
             dz_13 = dz_of[g][0]
             count = cnt_pool.tile([P, gt, K], BF16, name="count")
             for t in range(gt):
+                nc.tensor.matmul(
+                    out=count[:, t, :], lhsT=three_halves[:], rhs=ones[:], start=True, stop=False
+                )
                 for q in range(3):
                     nc.tensor.matmul(
-                        out=count[:, t, :], lhsT=ident_bf16[:], rhs=dz_13[:, q, t, :],
-                        start=(q == 0), stop=(q == 2),
+                        out=count[:, t, :], lhsT=minus_half[:], rhs=dz_13[:, q, t, :],
+                        start=False, stop=(q == 2),
                     )
-            share1 = work.tile([P, gt, K], BF16, name="share1")
-            nc.scalar.activation(out=share1[:], in_=count[:], func=ACT.Copy, scale=-0.5, bias=1.5)
-            share1_of[g] = share1
+            count_of[g] = count
+            share1_of[g] = work.tile([P, gt, K], BF16, name="share1")
 
         def early_products(g):
             gt = GROUP_TILES[g]
@@ -225,7 +240,8 @@ def tile_vrtconv_t_v_kernel(
             share2 = share2_of[g]
             nc.vector.tensor_tensor(out=share2[:], in0=share2[:], in1=grad[:, 1], op=ALU.mult)
             nc.vector.scalar_tensor_tensor(
-                out=share1, in0=share1, scalar=1.0 / 3.0, in1=grad[:, 0], op0=ALU.max, op1=ALU.mult
+                out=share1, in0=count_of[g][:].rearrange("p t k -> p (t k)"), scalar=1.0 / 3.0,
+                in1=grad[:, 0], op0=ALU.max, op1=ALU.mult,
             )
             nc.vector.tensor_tensor(
                 out=planes_2, in0=planes_2,
@@ -306,7 +322,7 @@ def tile_vrtconv_t_v_kernel(
                     in_=acc[l][:].rearrange("p (c d) -> p c d", d=D),
                 )
             if place == unit_tiles - 1:
-                nc.scalar.dma_start(
+                nc.sync.dma_start(
                     out=out_view[:, :, unit_first : unit_first + unit_tiles, :],
                     in_=staged[:].rearrange("p c t l d -> p c t (l d)"),
                 )

@@ -34,6 +34,7 @@ assert sum(GROUP_TILES) == TILES
 
 LOAD_BUFS = 3
 GRAD_TILES = 2
+GRAD_UNITS = {0: 2, 2: 2, 4: 2, 6: 2}
 STORE_UNITS = ((0, 1), (2,), (3,), (4,), (5,))
 
 WEIGHT_BATCHES = ((1, 2), (3,))
@@ -42,6 +43,10 @@ WEIGHT_BLOCKS = 6
 
 PASSES = [(2, p, a) for p in range(2) for a in range(2)] + [
     one_pass for l in range(L) for one_pass in ((1, l, 0), (3, 0, l))
+]
+
+LAST_PASSES = [(2, p, a) for p in range(2) for a in range(2)] + [
+    (3, 0, 0), (1, 0, 0), (3, 0, 1), (3, 0, 2), (1, 1, 0), (1, 2, 0),
 ]
 
 FLOPS = 2 * K * S * N_COLS * len(PASSES)
@@ -86,9 +91,9 @@ def tile_vrtconv_t_v_kernel(
         ident_bf16 = keep.tile([P, P], BF16)
         make_identity(nc, ident_bf16[:])
         minus_half = keep.tile([P, P], BF16)
-        nc.vector.tensor_scalar_mul(out=minus_half[:], in0=ident_bf16[:], scalar1=-0.5)
+        nc.vector.tensor_scalar(out=minus_half[:], in0=ident_bf16[:], scalar1=-0.5, scalar2=None, op0=ALU.mult)
         three_halves = keep.tile([P, P], BF16)
-        nc.vector.tensor_scalar_mul(out=three_halves[:], in0=ident_bf16[:], scalar1=1.5)
+        nc.vector.tensor_scalar(out=three_halves[:], in0=ident_bf16[:], scalar1=1.5, scalar2=None, op0=ALU.mult)
         ones = keep.tile([P, K], BF16)
         nc.vector.memset(ones[:], 1.0)
 
@@ -100,24 +105,32 @@ def tile_vrtconv_t_v_kernel(
         w_scales = keep.tile([P, WEIGHT_BLOCKS, N_COLS], U8, align_bytes=64)
 
         z_of, g_sorted_of, dz_of, share1_of, share2_of = {}, {}, {}, {}, {}
-        grouped_of, quantised_of, staged_of, count_of = {}, {}, {}, {}
+        grouped_of, quantised_of, staged_of, bank_of, acc_of, count_of = {}, {}, {}, {}, {}, {}
 
-        def load_group(g):
+        def load_group(g, order="abcgd"):
             gt = GROUP_TILES[g]
-            z = {h: loads.tile([P, L - h + 1, gt, K], F32, name="z%d" % h) for h in (1, 2, 3)}
+            if g not in z_of:
+                z_of[g] = {h: loads.tile([P, L - h + 1, gt, K], F32, name="z%d" % h) for h in (1, 2, 3)}
+            z = z_of[g]
             first = tiles_of(g).start
-            nc.sync.dma_start(out=z[1][:, 0:2], in_=conv_views[1][:, 0:2, tiles_of(g), :])
-            nc.sync.dma_start(out=z[2][:], in_=conv_views[2][:, :, tiles_of(g), :])
-            nc.sync.dma_start(out=z[1][:, 2:3], in_=conv_views[1][:, 2:3, tiles_of(g), :])
-            if first % GRAD_TILES == 0:
-                g_raw = loads.tile([P, C_CH, GRAD_TILES, J, L], BF16, name="g_raw")
-                nc.sync.dma_start(
-                    out=g_raw[:].rearrange("p o t j h -> p o t (j h)"),
-                    in_=grad_view[:, :, first : first + GRAD_TILES, :],
-                )
-                g_unit_of[first // GRAD_TILES] = g_raw
-            nc.sync.dma_start(out=z[3][:], in_=conv_views[3][:, :, tiles_of(g), :])
-            z_of[g] = z
+            for piece in order:
+                if piece == "a":
+                    nc.sync.dma_start(out=z[1][:, 0:2], in_=conv_views[1][:, 0:2, tiles_of(g), :])
+                if piece == "b":
+                    nc.sync.dma_start(out=z[2][:], in_=conv_views[2][:, :, tiles_of(g), :])
+                if piece == "c":
+                    nc.sync.dma_start(out=z[1][:, 2:3], in_=conv_views[1][:, 2:3, tiles_of(g), :])
+                if piece == "d":
+                    nc.sync.dma_start(out=z[3][:], in_=conv_views[3][:, :, tiles_of(g), :])
+                if piece == "g" and first in GRAD_UNITS:
+                    n_tiles = GRAD_UNITS[first]
+                    g_raw = loads.tile([P, C_CH, n_tiles, J, L], BF16, name="g_raw")
+                    nc.sync.dma_start(
+                        out=g_raw[:].rearrange("p o t j h -> p o t (j h)"),
+                        in_=grad_view[:, :, first : first + n_tiles, :],
+                    )
+                    for t in range(n_tiles):
+                        g_unit_of[first + t] = (g_raw, t)
 
         def load_weight(h):
             if h != 2:
@@ -131,69 +144,125 @@ def tile_vrtconv_t_v_kernel(
                     in_=rows[u * 2 * P : (u + 1) * 2 * P, :].rearrange("(p e) n -> p e n", e=2),
                 )
 
-        def regroup_weights(heights):
-            for h in heights:
+        def regroup_weights(blocks, copy):
+            for block in blocks:
+                h = [h for h in (1, 2, 3) if first_weight_block(h) <= block][-1]
                 by_kernel_row = w_raw[h].rearrange("p t (c a d) -> p a c d t", a=h, d=D)
-                for a in range(h):
-                    grouped = wstage.tile([P, C_CH, D, 4], BF16, align_bytes=64, name="w_grouped")
-                    nc.scalar.copy(out=grouped[:], in_=by_kernel_row[:, a])
-                    w_grouped[first_weight_block(h) + a] = grouped
+                grouped = wstage.tile([P, C_CH, D, 4], BF16, align_bytes=64, name="w_grouped")
+                copy(out=grouped[:], in_=by_kernel_row[:, block - first_weight_block(h)])
+                w_grouped[block] = grouped
 
-        def quantise_weights(heights):
-            for h in heights:
-                for block in range(first_weight_block(h), first_weight_block(h) + h):
-                    nc.vector.quantize_mx(
-                        out=w_codes[:, block, :].bitcast(E4M3_X4),
-                        scales=w_scales[:, block, :],
-                        in_=w_grouped[block][:].rearrange("p c d t -> p (c d t)"),
-                    )
+        def quantise_weights(blocks):
+            for block in blocks:
+                nc.vector.quantize_mx(
+                    out=w_codes[:, block, :].bitcast(E4M3_X4),
+                    scales=w_scales[:, block, :],
+                    in_=w_grouped[block][:].rearrange("p c d t -> p (c d t)"),
+                )
 
-        def sort_grad(g):
-            g_sorted = work.tile([P, L, GROUP_TILES[g], K], BF16, name="g_sorted")
-            unit, offset = divmod(tiles_of(g).start, GRAD_TILES)
-            g_raw = g_unit_of[unit]
-            if g > 0 and GROUP_TILES[g] == 1:
+        def sort_grad(g, heights=(3, 2, 1)):
+            if g not in g_sorted_of:
+                g_sorted_of[g] = work.tile([P, L, GROUP_TILES[g], K], BF16, name="g_sorted")
+            g_sorted = g_sorted_of[g]
+            g_raw, offset = g_unit_of[tiles_of(g).start]
+            if GROUP_TILES[g] == 1 and len(heights) == L:
                 nc.scalar.copy(
                     out=g_sorted[:, :, 0, :].rearrange("p h (b i o) -> p h b o i", i=4, o=C_CH),
                     in_=g_raw[:, :, offset, :, :].rearrange("p o (b i) h -> p h b o i", i=4),
                 )
             else:
-                for h in (3, 2, 1):
+                for h in heights:
                     nc.scalar.copy(
                         out=g_sorted[:, h - 1].rearrange("p t (b i o) -> p t b o i", i=4, o=C_CH),
                         in_=g_raw[:, :, offset : offset + GROUP_TILES[g], :, h - 1].rearrange(
                             "p o t (b i) -> p t b o i", i=4
                         ),
                     )
-            g_sorted_of[g] = g_sorted
 
-        def hits(g):
+        def vector_steps(g):
             gt = GROUP_TILES[g]
             z1 = z_of[g][1][:].rearrange("p q t k -> p q (t k)")
             z2 = z_of[g][2][:].rearrange("p q t k -> p q (t k)")
+            z3 = z_of[g][3][:].rearrange("p q t k -> p (q t k)")
             dz_13 = work.tile([P, 4, gt, K], BF16, name="dz_13")
             dz_2 = work.tile([P, 2, gt, K], BF16, name="dz_2")
             planes_13 = dz_13[:].rearrange("p q t k -> p q (t k)")
             planes_2 = dz_2[:].rearrange("p q t k -> p q (t k)")
             top = work.tile([P, gt * K], F32, name="top")
-            nc.vector.scalar_tensor_tensor(
-                out=top[:], in0=z1[:, 0], scalar=SMALLEST_NORMAL, in1=z1[:, 1],
-                op0=ALU.max, op1=ALU.max,
-            )
-            nc.vector.scalar_tensor_tensor(
-                out=planes_2[:, 0], in0=z2[:, 1], scalar=SMALLEST_NORMAL, in1=z2[:, 0],
-                op0=ALU.max, op1=ALU.is_le,
-            )
-            nc.vector.tensor_tensor(out=top[:], in0=top[:], in1=z1[:, 2], op=ALU.max)
-            nc.vector.scalar_tensor_tensor(
-                out=planes_2[:, 1], in0=z2[:, 0], scalar=SMALLEST_NORMAL, in1=z2[:, 1],
-                op0=ALU.max, op1=ALU.is_le,
-            )
-            nc.vector.tensor_tensor(
-                out=planes_13[:, 0:3], in0=z1,
-                in1=top[:].unsqueeze(1).to_broadcast([P, 3, gt * K]), op=ALU.is_ge,
-            )
+            share2 = work.tile([P, gt * K], BF16, name="share2")
             dz_of[g] = (dz_13, dz_2)
+
+            def grad(h):
+                return g_sorted_of[g][:].rearrange("p h t k -> p h (t k)")[:, h - 1]
+
+            def share1():
+                return share1_of[g][:].rearrange("p t k -> p (t k)")
+
+            def top_a():
+                nc.vector.scalar_tensor_tensor(
+                    out=top[:], in0=z1[:, 0], scalar=SMALLEST_NORMAL, in1=z1[:, 1],
+                    op0=ALU.max, op1=ALU.max,
+                )
+
+            def top_b():
+                nc.vector.tensor_tensor(out=top[:], in0=top[:], in1=z1[:, 2], op=ALU.max)
+
+            def mask2(q):
+                nc.vector.scalar_tensor_tensor(
+                    out=planes_2[:, q], in0=z2[:, 1 - q], scalar=SMALLEST_NORMAL, in1=z2[:, q],
+                    op0=ALU.max, op1=ALU.is_le,
+                )
+
+            def mask1():
+                nc.vector.tensor_tensor(
+                    out=planes_13[:, 1:4], in0=z1,
+                    in1=top[:].unsqueeze(1).to_broadcast([P, 3, gt * K]), op=ALU.is_ge,
+                )
+
+            def count2():
+                nc.vector.tensor_tensor(
+                    out=share2[:], in0=planes_2[:, 0], in1=planes_2[:, 1], op=ALU.add
+                )
+
+            def inverse2():
+                nc.vector.tensor_scalar(
+                    out=share2[:], in0=share2[:], scalar1=-0.5, scalar2=1.5,
+                    op0=ALU.mult, op1=ALU.add,
+                )
+
+            def grad_share2():
+                nc.vector.tensor_tensor(out=share2[:], in0=share2[:], in1=grad(2), op=ALU.mult)
+
+            def grad_share1():
+                nc.vector.scalar_tensor_tensor(
+                    out=share1(), in0=count_of[g][:].rearrange("p t k -> p (t k)"), scalar=1.0 / 3.0, in1=grad(1),
+                    op0=ALU.max, op1=ALU.mult,
+                )
+
+            def product3():
+                nc.vector.scalar_tensor_tensor(
+                    out=planes_13[:, 0], in0=z3, scalar=0.0, in1=grad(3),
+                    op0=ALU.is_gt, op1=ALU.mult,
+                )
+
+            def product2():
+                nc.vector.tensor_tensor(
+                    out=planes_2, in0=planes_2,
+                    in1=share2[:].unsqueeze(1).to_broadcast([P, 2, gt * K]), op=ALU.mult,
+                )
+
+            def product1(first, count):
+                nc.vector.tensor_tensor(
+                    out=planes_13[:, 1 + first : 1 + first + count],
+                    in0=planes_13[:, 1 + first : 1 + first + count],
+                    in1=share1().unsqueeze(1).to_broadcast([P, count, gt * K]), op=ALU.mult,
+                )
+
+            return {
+                "top_a": top_a, "top_b": top_b, "mask2": mask2, "mask1": mask1, "count2": count2,
+                "inverse2": inverse2, "grad_share2": grad_share2, "grad_share1": grad_share1,
+                "product3": product3, "product2": product2, "product1": product1,
+            }
 
         def count_hits(g):
             gt = GROUP_TILES[g]
@@ -205,161 +274,220 @@ def tile_vrtconv_t_v_kernel(
                 )
                 for q in range(3):
                     nc.tensor.matmul(
-                        out=count[:, t, :], lhsT=minus_half[:], rhs=dz_13[:, q, t, :],
+                        out=count[:, t, :], lhsT=minus_half[:], rhs=dz_13[:, 1 + q, t, :],
                         start=False, stop=(q == 2),
                     )
             count_of[g] = count
             share1_of[g] = work.tile([P, gt, K], BF16, name="share1")
 
-        def early_products(g):
-            gt = GROUP_TILES[g]
-            dz_13, dz_2 = dz_of[g]
-            planes_13 = dz_13[:].rearrange("p q t k -> p q (t k)")
-            planes_2 = dz_2[:].rearrange("p q t k -> p q (t k)")
-            grad = g_sorted_of[g][:].rearrange("p h t k -> p h (t k)")
-            z3 = z_of[g][3][:].rearrange("p q t k -> p (q t k)")
-            share2 = work.tile([P, gt * K], BF16, name="share2")
-            nc.vector.tensor_tensor(
-                out=share2[:], in0=planes_2[:, 0], in1=planes_2[:, 1], op=ALU.add
-            )
-            nc.vector.scalar_tensor_tensor(
-                out=planes_13[:, 3], in0=z3, scalar=0.0, in1=grad[:, 2], op0=ALU.is_gt, op1=ALU.mult,
-            )
-            nc.vector.tensor_scalar(
-                out=share2[:], in0=share2[:], scalar1=-0.5, scalar2=1.5, op0=ALU.mult, op1=ALU.add
-            )
-            share2_of[g] = share2
-
-        def late_products(g):
-            gt = GROUP_TILES[g]
-            dz_13, dz_2 = dz_of[g]
-            planes_13 = dz_13[:].rearrange("p q t k -> p q (t k)")
-            planes_2 = dz_2[:].rearrange("p q t k -> p q (t k)")
-            grad = g_sorted_of[g][:].rearrange("p h t k -> p h (t k)")
-            share1 = share1_of[g][:].rearrange("p t k -> p (t k)")
-            share2 = share2_of[g]
-            nc.vector.tensor_tensor(out=share2[:], in0=share2[:], in1=grad[:, 1], op=ALU.mult)
-            nc.vector.scalar_tensor_tensor(
-                out=share1, in0=count_of[g][:].rearrange("p t k -> p (t k)"), scalar=1.0 / 3.0,
-                in1=grad[:, 0], op0=ALU.max, op1=ALU.mult,
-            )
-            nc.vector.tensor_tensor(
-                out=planes_2, in0=planes_2,
-                in1=share2[:].unsqueeze(1).to_broadcast([P, 2, gt * K]), op=ALU.mult,
-            )
-            nc.vector.tensor_tensor(
-                out=planes_13[:, 0:3], in0=planes_13[:, 0:3],
-                in1=share1.unsqueeze(1).to_broadcast([P, 3, gt * K]), op=ALU.mult,
-            )
+        def transpose_slot(g, label, slot):
+            dz, planes = (dz_of[g][1], 2) if label == "2" else (dz_of[g][0], 4)
+            slots = GROUP_TILES[g] * planes
+            if slot == 0:
+                grouped_of[g, label] = work.tile(
+                    [P, slots, P, 4], BF16, align_bytes=64, name="grouped_" + label
+                )
+            if slot % 2 == 0:
+                bank_of[g, label] = xt_pool.tile([P, 2, 2, P], F32, name="xt")
+            xt = bank_of[g, label]
+            t, q = divmod(slot, planes)
+            words = dz[:, q, t, :].bitcast(F32)
+            for u in range(2):
+                nc.tensor.transpose(
+                    out=xt[:, slot % 2, u, :], in_=words[:, u * P : (u + 1) * P],
+                    identity=ident_f32[:],
+                )
+            if slot % 2 == 1:
+                grouped_words = grouped_of[g, label][:].bitcast(F32)
+                nc.scalar.copy(
+                    out=grouped_words[:, slot - 1 : slot + 1],
+                    in_=xt[:].rearrange("p i u s -> p i s u"),
+                )
 
         def transpose(g):
-            grouped_of[g] = {}
-            dz_13, dz_2 = dz_of[g]
-            for dz, planes, label in ((dz_2, 2, "2"), (dz_13, 4, "13")):
-                slots = GROUP_TILES[g] * planes
-                grouped = work.tile([P, slots, P, 4], BF16, align_bytes=64, name="grouped_" + label)
-                grouped_words = grouped[:].bitcast(F32)
-                for pair in range(slots // 2):
-                    xt = xt_pool.tile([P, 2, 2, P], F32, name="xt")
-                    for i in range(2):
-                        t, q = divmod(2 * pair + i, planes)
-                        words = dz[:, q, t, :].bitcast(F32)
-                        for u in range(2):
-                            nc.tensor.transpose(
-                                out=xt[:, i, u, :], in_=words[:, u * P : (u + 1) * P],
-                                identity=ident_f32[:],
-                            )
-                    nc.scalar.copy(
-                        out=grouped_words[:, 2 * pair : 2 * pair + 2],
-                        in_=xt[:].rearrange("p i u s -> p i s u"),
-                    )
-                grouped_of[g][label] = grouped
+            for label, planes in (("2", 2), ("13", 4)):
+                for slot in range(GROUP_TILES[g] * planes):
+                    transpose_slot(g, label, slot)
 
-        def quantise(g):
-            quantised_of[g] = {}
-            for label in ("2", "13"):
-                grouped = grouped_of[g][label]
-                slots = grouped.shape[1]
-                codes = work.tile([P, slots, P], U32, align_bytes=64, name="codes_" + label)
-                scales = work.tile([P, slots, P], U8, align_bytes=64, name="scales_" + label)
-                nc.vector.quantize_mx(
-                    out=codes[:].rearrange("p n s -> p (n s)").bitcast(E5M2_X4),
-                    scales=scales[:].rearrange("p n s -> p (n s)"),
-                    in_=grouped[:].rearrange("p n s t -> p (n s t)"),
+        def quantise(g, label, first=0, count=None):
+            grouped = grouped_of[g, label]
+            slots = grouped.shape[1]
+            if first == 0:
+                quantised_of[g, label] = (
+                    work.tile([P, slots, P], U32, align_bytes=64, name="codes_" + label),
+                    work.tile([P, slots, P], U8, align_bytes=64, name="scales_" + label),
                 )
-                quantised_of[g][label] = (codes, scales)
+            codes, scales = quantised_of[g, label]
+            some = slice(first, slots if count is None else first + count)
+            nc.vector.quantize_mx(
+                out=codes[:, some].rearrange("p n s -> p (n s)").bitcast(E5M2_X4),
+                scales=scales[:, some].rearrange("p n s -> p (n s)"),
+                in_=grouped[:, some].rearrange("p n s t -> p (n s t)"),
+            )
 
-        def multiply_tile(g, t):
-            gt = GROUP_TILES[g]
-            first_pass_of_row = {p + a: i for i, (h, p, a) in reversed(list(enumerate(PASSES)))}
+        def open_tile(g, t):
             unit = [groups for groups in STORE_UNITS if g in groups][0]
             unit_first = tiles_of(unit[0]).start
-            unit_tiles = tiles_of(unit[-1]).stop - unit_first
-            place = tiles_of(g).start + t - unit_first
-            if place == 0:
+            if tiles_of(g).start + t == unit_first:
+                unit_tiles = tiles_of(unit[-1]).stop - unit_first
                 staged_of[unit] = big.tile([P, C_CH, unit_tiles, L, D], F32, name="big")
-            staged = staged_of[unit]
-            acc = [acc_pool.tile([P, N_COLS], F32, name="acc%d" % l) for l in range(L)]
-            for i, (h, p, a) in enumerate(PASSES):
+            acc_of[g, t] = [acc_pool.tile([P, N_COLS], F32, name="acc%d" % l) for l in range(L)]
+
+        def run_passes(g, t, order, some):
+            first_of_row = {p + a: i for i, (h, p, a) in reversed(list(enumerate(order)))}
+            last_of_row = {p + a: i for i, (h, p, a) in enumerate(order)}
+            for i in some:
+                h, p, a = order[i]
                 if h == 2:
-                    (codes, scales), slot = quantised_of[g]["2"], t * 2 + p
+                    (codes, scales), slot = quantised_of[g, "2"], t * 2 + p
                 else:
-                    (codes, scales), slot = quantised_of[g]["13"], t * 4 + (p if h == 1 else 3)
+                    (codes, scales), slot = quantised_of[g, "13"], t * 4 + (1 + p if h == 1 else 0)
                 block = first_weight_block(h) + a
                 nc.tensor.matmul_mx(
-                    out=acc[p + a][:],
+                    out=acc_of[g, t][p + a][:],
                     lhsT=codes[:, slot, :].bitcast(E5M2_X4),
                     lhsT_scale=scales[:, slot, :],
                     rhs=w_codes[:, block, :].bitcast(E4M3_X4),
                     rhs_scale=w_scales[:, block, :],
-                    start=(i == first_pass_of_row[p + a]),
-                    stop=(h == 3),
+                    start=(i == first_of_row[p + a]),
+                    stop=(i == last_of_row[p + a]),
                 )
-            for l in range(L):
-                copy_out = nc.vector.tensor_copy if (g == GROUPS - 1 and l == 1) else nc.scalar.copy
-                copy_out(
-                    out=staged[:, :, place, l, :],
-                    in_=acc[l][:].rearrange("p (c d) -> p c d", d=D),
-                )
-            if place == unit_tiles - 1:
+
+        def empty_row(g, t, l, copy_out):
+            unit = [groups for groups in STORE_UNITS if g in groups][0]
+            copy_out(
+                out=staged_of[unit][:, :, tiles_of(g).start + t - tiles_of(unit[0]).start, l, :],
+                in_=acc_of[g, t][l][:].rearrange("p (c d) -> p c d", d=D),
+            )
+
+        def store_behind(g, t):
+            unit = [groups for groups in STORE_UNITS if g in groups][0]
+            if tiles_of(g).start + t == tiles_of(unit[-1]).stop - 1:
                 nc.sync.dma_start(
-                    out=out_view[:, :, unit_first : unit_first + unit_tiles, :],
-                    in_=staged[:].rearrange("p c t l d -> p c t (l d)"),
+                    out=out_view[:, :, tiles_of(unit[0]).start : tiles_of(unit[-1]).stop, :],
+                    in_=staged_of[unit][:].rearrange("p c t l d -> p c t (l d)"),
                 )
 
-        for g, batch in enumerate(WEIGHT_BATCHES):
-            load_group(g)
-            for h in batch:
-                load_weight(h)
-        for g in range(len(WEIGHT_BATCHES), LOAD_BUFS):
-            load_group(g)
-        sort_grad(0)
+        def multiply_tile(g, t):
+            open_tile(g, t)
+            run_passes(g, t, PASSES, range(len(PASSES)))
+            for l in range(L):
+                empty_row(g, t, l, nc.scalar.copy)
+            store_behind(g, t)
 
-        first_turn_of_products = len(WEIGHT_BATCHES)
+        load_group(0)
+        load_weight(1)
+        load_group(1, "abc")
+        load_weight(2)
+        load_group(1, "gd")
+        load_weight(3)
+        load_group(2)
+        sort_grad(0, (3, 2))
+
         due = []
-        for g in range(GROUPS):
-            hits(g)
+        step = vector_steps(0)
+        step["top_a"]()
+        step["mask2"](0)
+        step["top_b"]()
+        step["mask2"](1)
+        step["mask1"]()
+        count_hits(0)
+        sort_grad(0, (1,))
+
+        step["count2"]()
+        step["product3"]()
+        step["inverse2"]()
+        step["grad_share2"]()
+        step["grad_share1"]()
+        step["product2"]()
+        step["product1"](0, 3)
+        load_group(3)
+        sort_grad(1)
+        regroup_weights((0, 1), nc.scalar.copy)
+        transpose(0)
+
+        step = vector_steps(1)
+        step["top_a"]()
+        step["mask2"](0)
+        step["top_b"]()
+        step["mask2"](1)
+        step["mask1"]()
+        count_hits(1)
+        step["count2"]()
+        step["product3"]()
+        step["inverse2"]()
+        regroup_weights((2,), nc.vector.tensor_copy)
+        quantise_weights((0, 1, 2))
+        quantise(0, "2")
+        quantise(0, "13")
+        due.append((0, 0))
+        regroup_weights((3, 4, 5), nc.scalar.copy)
+        sort_grad(2)
+        step["grad_share2"]()
+        step["grad_share1"]()
+        step["product2"]()
+        step["product1"](0, 3)
+        load_group(4)
+        transpose(1)
+
+        step = vector_steps(2)
+        step["top_a"]()
+        step["mask2"](0)
+        step["top_b"]()
+        step["mask2"](1)
+
+        step["mask1"]()
+        count_hits(2)
+        step["count2"]()
+        step["product3"]()
+        step["inverse2"]()
+        quantise_weights((3, 4, 5))
+        quantise(1, "2")
+        quantise(1, "13")
+        due.append((1, 0))
+        sort_grad(3)
+        multiply_tile(*due[0])
+        step["grad_share2"]()
+        step["grad_share1"]()
+        step["product2"]()
+        step["product1"](0, 3)
+        load_group(5)
+        transpose(2)
+        multiply_tile(*due[1])
+        due = []
+        for g in range(3, GROUPS):
+            step = vector_steps(g)
+            step["top_a"]()
+            step["mask2"](0)
+            step["top_b"]()
+            step["mask2"](1)
+            step["mask1"]()
             count_hits(g)
-            early_products(g)
-            if 1 <= g <= len(WEIGHT_BATCHES):
-                quantise_weights(WEIGHT_BATCHES[g - 1])
-            if g >= 1:
-                quantise(g - 1)
-                due.extend([(g - 1, t) for t in range(GROUP_TILES[g - 1])])
-            if g < len(WEIGHT_BATCHES):
-                regroup_weights(WEIGHT_BATCHES[g])
+            step["count2"]()
+            step["product3"]()
+            step["inverse2"]()
+            quantise(g - 1, "2")
+            quantise(g - 1, "13")
+            due.extend([(g - 1, t) for t in range(GROUP_TILES[g - 1])])
             if g + 1 < GROUPS:
                 sort_grad(g + 1)
-            if g >= first_turn_of_products:
-                multiply_tile(*due[0])
-            late_products(g)
+            multiply_tile(*due[0])
+            step["grad_share2"]()
+            step["grad_share1"]()
+            step["product2"]()
+            step["product1"](0, 3)
             if g + LOAD_BUFS < GROUPS:
                 load_group(g + LOAD_BUFS)
             transpose(g)
-            if g >= first_turn_of_products:
-                for group_and_tile in due[1:]:
-                    multiply_tile(*group_and_tile)
-                due = []
-        quantise(GROUPS - 1)
-        for t in range(GROUP_TILES[GROUPS - 1]):
-            multiply_tile(GROUPS - 1, t)
+            for group_and_tile in due[1:]:
+                multiply_tile(*group_and_tile)
+            due = []
+        g = GROUPS - 1
+        quantise(g, "2")
+        quantise(g, "13")
+        open_tile(g, 0)
+        run_passes(g, 0, PASSES, range(len(PASSES)))
+        empty_row(g, 0, 0, nc.scalar.copy)
+        empty_row(g, 0, 1, nc.vector.tensor_copy)
+        empty_row(g, 0, 2, nc.scalar.copy)
+        store_behind(g, 0)

@@ -280,7 +280,7 @@ def tile_vrtconv_t_v_kernel(
             count_of[g] = count
             share1_of[g] = work.tile([P, gt, K], BF16, name="share1")
 
-        def transpose_slot(g, label, slot):
+        def transpose_slot(g, label, slot, copy=None):
             dz, planes = (dz_of[g][1], 2) if label == "2" else (dz_of[g][0], 4)
             slots = GROUP_TILES[g] * planes
             if slot == 0:
@@ -299,7 +299,7 @@ def tile_vrtconv_t_v_kernel(
                 )
             if slot % 2 == 1:
                 grouped_words = grouped_of[g, label][:].bitcast(F32)
-                nc.scalar.copy(
+                (copy or nc.scalar.copy)(
                     out=grouped_words[:, slot - 1 : slot + 1],
                     in_=xt[:].rearrange("p i u s -> p i s u"),
                 )
@@ -401,7 +401,7 @@ def tile_vrtconv_t_v_kernel(
         step["grad_share1"]()
         step["product2"]()
         step["product1"](0, 3)
-        load_group(3)
+        load_group(3, "gabcd")
         sort_grad(1)
         regroup_weights((0, 1), nc.scalar.copy)
         transpose(0)
@@ -455,22 +455,40 @@ def tile_vrtconv_t_v_kernel(
         transpose(2)
         multiply_tile(*due[1])
         due = []
-        for g in range(3, GROUPS):
+        def rows_and_store(g, t):
+            for l in range(L):
+                empty_row(g, t, l, nc.scalar.copy)
+            store_behind(g, t)
+
+        for g in range(3, GROUPS - 1):
+            early = g >= 99
             step = vector_steps(g)
             step["top_a"]()
             step["mask2"](0)
             step["top_b"]()
+            if GROUP_TILES[g - 1] == 2 and g >= 3:
+                quantise(g - 1, "2", 0, 2)
+                quantise(g - 1, "13", 0, 4)
+                multiply_tile(g - 1, 0)
             step["mask2"](1)
+            pass
             step["mask1"]()
             count_hits(g)
+            if early:
+                quantise(g - 1, "2")
+                quantise(g - 1, "13")
             step["count2"]()
             step["product3"]()
             step["inverse2"]()
-            quantise(g - 1, "2")
-            quantise(g - 1, "13")
-            due.extend([(g - 1, t) for t in range(GROUP_TILES[g - 1])])
-            if g + 1 < GROUPS:
-                sort_grad(g + 1)
+            if GROUP_TILES[g - 1] == 2 and g >= 3:
+                quantise(g - 1, "2", 2, 2)
+                quantise(g - 1, "13", 4, 4)
+                due.append((g - 1, 1))
+            else:
+                quantise(g - 1, "2")
+                quantise(g - 1, "13")
+                due.extend([(g - 1, t) for t in range(GROUP_TILES[g - 1])])
+            sort_grad(g + 1)
             multiply_tile(*due[0])
             step["grad_share2"]()
             step["grad_share1"]()
@@ -483,11 +501,41 @@ def tile_vrtconv_t_v_kernel(
                 multiply_tile(*group_and_tile)
             due = []
         g = GROUPS - 1
+        step = vector_steps(g)
+        step["top_a"]()
+        step["mask2"](0)
+        step["top_b"]()
+        step["mask2"](1)
+        quantise(g - 1, "2")
+        quantise(g - 1, "13")
+        open_tile(g - 1, 0)
+        run_passes(g - 1, 0, PASSES, range(8))
+        step["mask1"]()
+        count_hits(g)
+        run_passes(g - 1, 0, PASSES, range(8, 10))
+        rows_and_store(g - 1, 0)
+        step["count2"]()
+        step["product3"]()
+        transpose_slot(g, "13", 0)
+        step["inverse2"]()
+        step["grad_share2"]()
+        step["product2"]()
+        transpose_slot(g, "2", 0)
+        transpose_slot(g, "2", 1)
+        step["grad_share1"]()
+        step["product1"](0, 1)
+        transpose_slot(g, "13", 1)
+        step["product1"](1, 2)
+        transpose_slot(g, "13", 2)
+        transpose_slot(g, "13", 3)
         quantise(g, "2")
-        quantise(g, "13")
         open_tile(g, 0)
-        run_passes(g, 0, PASSES, range(len(PASSES)))
+        run_passes(g, 0, LAST_PASSES, (0, 1, 2, 3))
+        quantise(g, "13", 0, 2)
+        run_passes(g, 0, LAST_PASSES, (4, 5, 6, 7))
         empty_row(g, 0, 0, nc.scalar.copy)
+        quantise(g, "13", 2, 2)
+        run_passes(g, 0, LAST_PASSES, (8, 9))
         empty_row(g, 0, 1, nc.vector.tensor_copy)
         empty_row(g, 0, 2, nc.scalar.copy)
         store_behind(g, 0)

from contextlib import ExitStack

from concourse import mybir
from concourse.masks import make_identity

F32 = mybir.dt.float32
BF16 = mybir.dt.bfloat16
U32 = mybir.dt.uint32
U8 = mybir.dt.uint8
E4M3_X4 = mybir.dt.float8_e4m3fn_x4
E5M2_X4 = mybir.dt.float8_e5m2_x4
ALU = mybir.AluOpType
ACT = mybir.ActivationFunctionType

P = 128
C_CH = 16
S = 1024
L = 3
D = 32
J = 32
K = J * C_CH
N_COLS = C_CH * D
TILES = S // P
SMALLEST_NORMAL = 2.0**-126

SINGLE_TILE_GROUPS_AT_EACH_END = 2
GROUP_TILES = (
    (1,) * SINGLE_TILE_GROUPS_AT_EACH_END
    + (2,) * ((TILES - 2 * SINGLE_TILE_GROUPS_AT_EACH_END) // 2)
    + (1,) * SINGLE_TILE_GROUPS_AT_EACH_END
)
GROUPS = len(GROUP_TILES)
assert sum(GROUP_TILES) == TILES

LOAD_BUFS = 3
GRAD_TILES = 2
GRAD_UNITS = {0: 2, 2: 2, 4: 2, 6: 2}
STORE_UNITS = ((0, 1), (2,), (3,), (4,), (5,))

WEIGHT_BATCHES = ((1, 2), (3,))
BLOCKS_IN_A_BATCH = 3
WEIGHT_BLOCKS = 6

PASSES = [(2, p, a) for p in range(2) for a in range(2)] + [
    one_pass for l in range(L) for one_pass in ((1, l, 0), (3, 0, l))
]

LAST_PASSES = [(2, p, a) for p in range(2) for a in range(2)] + [
    (3, 0, 0), (1, 0, 0), (3, 0, 1), (3, 0, 2), (1, 1, 0), (1, 2, 0),
]

FLOPS = 2 * K * S * N_COLS * len(PASSES)
BYTES = 4 * 6 * S * K + 2 * C_CH * S * L * J + 2 * K * N_COLS * WEIGHT_BLOCKS + 4 * C_CH * S * L * D


def first_weight_block(h):
    return h * (h - 1) // 2


def tile_vrtconv_t_v_kernel(
    tc, Ec, W1, W2, W3, b1, b2, b3, conv1, conv2, conv3, grad_out, out
):
    nc = tc.nc
    weights = {1: W1, 2: W2, 3: W3}

    conv_views = {
        1: conv1.rearrange("q (p t) j o -> p q t (j o)", t=TILES),
        2: conv2.rearrange("q (p t) j o -> p q t (j o)", t=TILES),
        3: conv3.rearrange("q (p t) j o -> p q t (j o)", t=TILES),
    }
    grad_view = grad_out.rearrange("o (p t) x i -> p o t (x i)", t=TILES)
    out_view = out.rearrange("c (p t) l d -> p c t (l d)", t=TILES)

    def tiles_of(g):
        first = sum(GROUP_TILES[:g])
        return slice(first, first + GROUP_TILES[g])

    with ExitStack() as stack:
        keep = stack.enter_context(tc.tile_pool(name="keep", bufs=1))
        wstage = stack.enter_context(tc.tile_pool(name="wstage", bufs=BLOCKS_IN_A_BATCH))
        loads = stack.enter_context(tc.tile_pool(name="loads", bufs=LOAD_BUFS))
        big = stack.enter_context(tc.tile_pool(name="big", bufs=2))
        work = stack.enter_context(tc.tile_pool(name="work", bufs=2))
        acc_pool = stack.enter_context(tc.psum_pool(name="acc", bufs=1))
        xt_pool = stack.enter_context(tc.psum_pool(name="xt", bufs=4))
        cnt_pool = stack.enter_context(tc.psum_pool(name="cnt", bufs=1))
        stack.enter_context(tc.manual_schedule())

        ident_f32 = keep.tile([P, P], F32)
        make_identity(nc, ident_f32[:])
        ident_bf16 = keep.tile([P, P], BF16)
        make_identity(nc, ident_bf16[:])
        minus_half = keep.tile([P, P], BF16)
        nc.vector.tensor_scalar(out=minus_half[:], in0=ident_bf16[:], scalar1=-0.5, scalar2=None, op0=ALU.mult)
        three_halves = keep.tile([P, P], BF16)
        nc.vector.tensor_scalar(out=three_halves[:], in0=ident_bf16[:], scalar1=1.5, scalar2=None, op0=ALU.mult)
        ones = keep.tile([P, K], BF16)
        nc.vector.memset(ones[:], 1.0)

        w_raw = {}
        w_tile = [None]
        g_unit_of = {}
        w_grouped = {}
        w_codes = keep.tile([P, WEIGHT_BLOCKS, N_COLS], U32, align_bytes=64)
        w_scales = keep.tile([P, WEIGHT_BLOCKS, N_COLS], U8, align_bytes=64)

        z_of, g_sorted_of, dz_of, share1_of, share2_of = {}, {}, {}, {}, {}
        grouped_of, quantised_of, staged_of, bank_of, acc_of, count_of = {}, {}, {}, {}, {}, {}

        def load_group(g, order="abcgd"):
            gt = GROUP_TILES[g]
            if g not in z_of:
                z_of[g] = {h: loads.tile([P, L - h + 1, gt, K], F32, name="z%d" % h) for h in (1, 2, 3)}
            z = z_of[g]
            first = tiles_of(g).start
            for piece in order:
                if piece == "a":
                    nc.sync.dma_start(out=z[1][:, 0:2], in_=conv_views[1][:, 0:2, tiles_of(g), :])
                if piece == "b":
                    nc.sync.dma_start(out=z[2][:], in_=conv_views[2][:, :, tiles_of(g), :])
                if piece == "c":
                    nc.sync.dma_start(out=z[1][:, 2:3], in_=conv_views[1][:, 2:3, tiles_of(g), :])
                if piece == "d":
                    nc.sync.dma_start(out=z[3][:], in_=conv_views[3][:, :, tiles_of(g), :])
                if piece == "g" and first in GRAD_UNITS:
                    n_tiles = GRAD_UNITS[first]
                    g_raw = loads.tile([P, C_CH, n_tiles, J, L], BF16, name="g_raw")
                    nc.sync.dma_start(
                        out=g_raw[:].rearrange("p o t j h -> p o t (j h)"),
                        in_=grad_view[:, :, first : first + n_tiles, :],
                    )
                    for t in range(n_tiles):
                        g_unit_of[first + t] = (g_raw, t)

        def load_weight(h):
            if h != 2:
                w_tile[0] = big.tile([P, 4, 3 * N_COLS], BF16, name="big")
            first_col = N_COLS if h == 2 else 0
            w_raw[h] = w_tile[0][:, :, first_col : first_col + h * N_COLS]
            rows = weights[h].rearrange("j o c a d -> (j o) (c a d)")
            for u in range(2):
                nc.sync.dma_start(
                    out=w_raw[h][:, 2 * u : 2 * u + 2, :],
                    in_=rows[u * 2 * P : (u + 1) * 2 * P, :].rearrange("(p e) n -> p e n", e=2),
                )

        def regroup_weights(blocks, copy):
            for block in blocks:
                h = [h for h in (1, 2, 3) if first_weight_block(h) <= block][-1]
                by_kernel_row = w_raw[h].rearrange("p t (c a d) -> p a c d t", a=h, d=D)
                grouped = wstage.tile([P, C_CH, D, 4], BF16, align_bytes=64, name="w_grouped")
                copy(out=grouped[:], in_=by_kernel_row[:, block - first_weight_block(h)])
                w_grouped[block] = grouped

        def quantise_weights(blocks):
            for block in blocks:
                nc.vector.quantize_mx(
                    out=w_codes[:, block, :].bitcast(E4M3_X4),
                    scales=w_scales[:, block, :],
                    in_=w_grouped[block][:].rearrange("p c d t -> p (c d t)"),
                )

        def sort_grad(g, heights=(3, 2, 1)):
            if g not in g_sorted_of:
                g_sorted_of[g] = work.tile([P, L, GROUP_TILES[g], K], BF16, name="g_sorted")
            g_sorted = g_sorted_of[g]
            g_raw, offset = g_unit_of[tiles_of(g).start]
            if GROUP_TILES[g] == 1 and len(heights) == L:
                nc.scalar.copy(
                    out=g_sorted[:, :, 0, :].rearrange("p h (b i o) -> p h b o i", i=4, o=C_CH),
                    in_=g_raw[:, :, offset, :, :].rearrange("p o (b i) h -> p h b o i", i=4),
                )
            else:
                for h in heights:
                    nc.scalar.copy(
                        out=g_sorted[:, h - 1].rearrange("p t (b i o) -> p t b o i", i=4, o=C_CH),
                        in_=g_raw[:, :, offset : offset + GROUP_TILES[g], :, h - 1].rearrange(
                            "p o t (b i) -> p t b o i", i=4
                        ),
                    )

        def vector_steps(g):
            gt = GROUP_TILES[g]
            z1 = z_of[g][1][:].rearrange("p q t k -> p q (t k)")
            z2 = z_of[g][2][:].rearrange("p q t k -> p q (t k)")
            z3 = z_of[g][3][:].rearrange("p q t k -> p (q t k)")
            dz_13 = work.tile([P, 4, gt, K], BF16, name="dz_13")
            dz_2 = work.tile([P, 2, gt, K], BF16, name="dz_2")
            planes_13 = dz_13[:].rearrange("p q t k -> p q (t k)")
            planes_2 = dz_2[:].rearrange("p q t k -> p q (t k)")
            top = work.tile([P, gt * K], F32, name="top")
            share2 = work.tile([P, gt * K], BF16, name="share2")
            dz_of[g] = (dz_13, dz_2)

            def grad(h):
                return g_sorted_of[g][:].rearrange("p h t k -> p h (t k)")[:, h - 1]

            def share1():
                return share1_of[g][:].rearrange("p t k -> p (t k)")

            def top_a():
                nc.vector.scalar_tensor_tensor(
                    out=top[:], in0=z1[:, 0], scalar=SMALLEST_NORMAL, in1=z1[:, 1],
                    op0=ALU.max, op1=ALU.max,
                )

            def top_b():
                nc.vector.tensor_tensor(out=top[:], in0=top[:], in1=z1[:, 2], op=ALU.max)

            def mask2(q):
                nc.vector.scalar_tensor_tensor(
                    out=planes_2[:, q], in0=z2[:, 1 - q], scalar=SMALLEST_NORMAL, in1=z2[:, q],
                    op0=ALU.max, op1=ALU.is_le,
                )

            def mask1():
                nc.vector.tensor_tensor(
                    out=planes_13[:, 1:4], in0=z1,
                    in1=top[:].unsqueeze(1).to_broadcast([P, 3, gt * K]), op=ALU.is_ge,
                )

            def count2():
                nc.vector.tensor_tensor(
                    out=share2[:], in0=planes_2[:, 0], in1=planes_2[:, 1], op=ALU.add
                )

            def inverse2():
                nc.vector.tensor_scalar(
                    out=share2[:], in0=share2[:], scalar1=-0.5, scalar2=1.5,
                    op0=ALU.mult, op1=ALU.add,
                )

            def grad_share2():
                nc.vector.tensor_tensor(out=share2[:], in0=share2[:], in1=grad(2), op=ALU.mult)

            def grad_share1():
                nc.vector.scalar_tensor_tensor(
                    out=share1(), in0=count_of[g][:].rearrange("p t k -> p (t k)"), scalar=1.0 / 3.0, in1=grad(1),
                    op0=ALU.max, op1=ALU.mult,
                )

            def product3():
                nc.vector.scalar_tensor_tensor(
                    out=planes_13[:, 0], in0=z3, scalar=0.0, in1=grad(3),
                    op0=ALU.is_gt, op1=ALU.mult,
                )

            def product2():
                nc.vector.tensor_tensor(
                    out=planes_2, in0=planes_2,
                    in1=share2[:].unsqueeze(1).to_broadcast([P, 2, gt * K]), op=ALU.mult,
                )

            def product1(first, count):
                nc.vector.tensor_tensor(
                    out=planes_13[:, 1 + first : 1 + first + count],
                    in0=planes_13[:, 1 + first : 1 + first + count],
                    in1=share1().unsqueeze(1).to_broadcast([P, count, gt * K]), op=ALU.mult,
                )

            return {
                "top_a": top_a, "top_b": top_b, "mask2": mask2, "mask1": mask1, "count2": count2,
                "inverse2": inverse2, "grad_share2": grad_share2, "grad_share1": grad_share1,
                "product3": product3, "product2": product2, "product1": product1,
            }

        def count_hits(g):
            gt = GROUP_TILES[g]
            dz_13 = dz_of[g][0]
            count = cnt_pool.tile([P, gt, K], BF16, name="count")
            for t in range(gt):
                nc.tensor.matmul(
                    out=count[:, t, :], lhsT=three_halves[:], rhs=ones[:], start=True, stop=False
                )
                for q in range(3):
                    nc.tensor.matmul(
                        out=count[:, t, :], lhsT=minus_half[:], rhs=dz_13[:, 1 + q, t, :],
                        start=False, stop=(q == 2),
                    )
            count_of[g] = count
            share1_of[g] = work.tile([P, gt, K], BF16, name="share1")

        def transpose_slot(g, label, slot, copy=None):
            dz, planes = (dz_of[g][1], 2) if label == "2" else (dz_of[g][0], 4)
            slots = GROUP_TILES[g] * planes
            if slot == 0:
                grouped_of[g, label] = work.tile(
                    [P, slots, P, 4], BF16, align_bytes=64, name="grouped_" + label
                )
            if slot % 2 == 0:
                bank_of[g, label] = xt_pool.tile([P, 2, 2, P], F32, name="xt")
            xt = bank_of[g, label]
            t, q = divmod(slot, planes)
            words = dz[:, q, t, :].bitcast(F32)
            for u in range(2):
                nc.tensor.transpose(
                    out=xt[:, slot % 2, u, :], in_=words[:, u * P : (u + 1) * P],
                    identity=ident_f32[:],
                )
            if slot % 2 == 1:
                grouped_words = grouped_of[g, label][:].bitcast(F32)
                (copy or nc.scalar.copy)(
                    out=grouped_words[:, slot - 1 : slot + 1],
                    in_=xt[:].rearrange("p i u s -> p i s u"),
                )

        def transpose(g):
            for label, planes in (("2", 2), ("13", 4)):
                for slot in range(GROUP_TILES[g] * planes):
                    transpose_slot(g, label, slot)

        def quantise(g, label, first=0, count=None):
            grouped = grouped_of[g, label]
            slots = grouped.shape[1]
            if first == 0:
                quantised_of[g, label] = (
                    work.tile([P, slots, P], U32, align_bytes=64, name="codes_" + label),
                    work.tile([P, slots, P], U8, align_bytes=64, name="scales_" + label),
                )
            codes, scales = quantised_of[g, label]
            some = slice(first, slots if count is None else first + count)
            nc.vector.quantize_mx(
                out=codes[:, some].rearrange("p n s -> p (n s)").bitcast(E5M2_X4),
                scales=scales[:, some].rearrange("p n s -> p (n s)"),
                in_=grouped[:, some].rearrange("p n s t -> p (n s t)"),
            )

        def open_tile(g, t):
            unit = [groups for groups in STORE_UNITS if g in groups][0]
            unit_first = tiles_of(unit[0]).start
            if tiles_of(g).start + t == unit_first:
                unit_tiles = tiles_of(unit[-1]).stop - unit_first
                staged_of[unit] = big.tile([P, C_CH, unit_tiles, L, D], F32, name="big")
            acc_of[g, t] = [acc_pool.tile([P, N_COLS], F32, name="acc%d" % l) for l in range(L)]

        def run_passes(g, t, order, some):
            first_of_row = {p + a: i for i, (h, p, a) in reversed(list(enumerate(order)))}
            last_of_row = {p + a: i for i, (h, p, a) in enumerate(order)}
            for i in some:
                h, p, a = order[i]
                if h == 2:
                    (codes, scales), slot = quantised_of[g, "2"], t * 2 + p
                else:
                    (codes, scales), slot = quantised_of[g, "13"], t * 4 + (1 + p if h == 1 else 0)
                block = first_weight_block(h) + a
                nc.tensor.matmul_mx(
                    out=acc_of[g, t][p + a][:],
                    lhsT=codes[:, slot, :].bitcast(E5M2_X4),
                    lhsT_scale=scales[:, slot, :],
                    rhs=w_codes[:, block, :].bitcast(E4M3_X4),
                    rhs_scale=w_scales[:, block, :],
                    start=(i == first_of_row[p + a]),
                    stop=(i == last_of_row[p + a]),
                )

        def empty_row(g, t, l, copy_out):
            unit = [groups for groups in STORE_UNITS if g in groups][0]
            copy_out(
                out=staged_of[unit][:, :, tiles_of(g).start + t - tiles_of(unit[0]).start, l, :],
                in_=acc_of[g, t][l][:].rearrange("p (c d) -> p c d", d=D),
            )

        def store_behind(g, t):
            unit = [groups for groups in STORE_UNITS if g in groups][0]
            if tiles_of(g).start + t == tiles_of(unit[-1]).stop - 1:
                nc.sync.dma_start(
                    out=out_view[:, :, tiles_of(unit[0]).start : tiles_of(unit[-1]).stop, :],
                    in_=staged_of[unit][:].rearrange("p c t l d -> p c t (l d)"),
                )

        def multiply_tile(g, t):
            open_tile(g, t)
            run_passes(g, t, PASSES, range(len(PASSES)))
            for l in range(L):
                empty_row(g, t, l, nc.scalar.copy)
            store_behind(g, t)

        load_group(0)
        load_weight(1)
        load_group(1, "abc")
        load_weight(2)
        load_group(1, "gd")
        load_weight(3)
        load_group(2)
        sort_grad(0, (3, 2))

        due = []
        step = vector_steps(0)
        step["top_a"]()
        step["mask2"](0)
        step["top_b"]()
        step["mask2"](1)
        step["mask1"]()
        count_hits(0)
        sort_grad(0, (1,))

        step["count2"]()
        step["product3"]()
        step["inverse2"]()
        step["grad_share2"]()
        step["grad_share1"]()
        step["product2"]()
        step["product1"](0, 3)
        load_group(3, "gabcd")
        sort_grad(1)
        regroup_weights((0, 1), nc.scalar.copy)
        transpose(0)

        step = vector_steps(1)
        step["top_a"]()
        step["mask2"](0)
        step["top_b"]()
        step["mask2"](1)
        step["mask1"]()
        count_hits(1)
        step["count2"]()
        step["product3"]()
        step["inverse2"]()
        regroup_weights((2,), nc.vector.tensor_copy)
        quantise_weights((0, 1, 2))
        quantise(0, "2")
        quantise(0, "13")
        due.append((0, 0))
        regroup_weights((3, 4, 5), nc.scalar.copy)
        sort_grad(2)
        step["grad_share2"]()
        step["grad_share1"]()
        step["product2"]()
        step["product1"](0, 3)
        load_group(4)
        transpose(1)

        step = vector_steps(2)
        step["top_a"]()
        step["mask2"](0)
        step["top_b"]()
        step["mask2"](1)

        step["mask1"]()
        count_hits(2)
        step["count2"]()
        step["product3"]()
        step["inverse2"]()
        quantise_weights((3, 4, 5))
        quantise(1, "2")
        quantise(1, "13")
        due.append((1, 0))
        sort_grad(3)
        multiply_tile(*due[0])
        step["grad_share2"]()
        step["grad_share1"]()
        step["product2"]()
        step["product1"](0, 3)
        load_group(5)
        transpose(2)
        multiply_tile(*due[1])
        due = []
        def rows_and_store(g, t):
            for l in range(L):
                empty_row(g, t, l, nc.scalar.copy)
            store_behind(g, t)

        for g in range(3, GROUPS - 1):
            early = g >= 99
            step = vector_steps(g)
            step["top_a"]()
            step["mask2"](0)
            step["top_b"]()
            if GROUP_TILES[g - 1] == 2 and g >= 3:
                quantise(g - 1, "2", 0, 2)
                quantise(g - 1, "13", 0, 4)
                multiply_tile(g - 1, 0)
            step["mask2"](1)
            pass
            step["mask1"]()
            count_hits(g)
            if early:
                quantise(g - 1, "2")
                quantise(g - 1, "13")
            step["count2"]()
            step["product3"]()
            step["inverse2"]()
            if GROUP_TILES[g - 1] == 2 and g >= 3:
                quantise(g - 1, "2", 2, 2)
                quantise(g - 1, "13", 4, 4)
                due.append((g - 1, 1))
            else:
                quantise(g - 1, "2")
                quantise(g - 1, "13")
                due.extend([(g - 1, t) for t in range(GROUP_TILES[g - 1])])
            sort_grad(g + 1)
            multiply_tile(*due[0])
            step["grad_share2"]()
            step["grad_share1"]()
            step["product2"]()
            step["product1"](0, 3)
            if g + LOAD_BUFS < GROUPS:
                load_group(g + LOAD_BUFS)
            transpose(g)
            for group_and_tile in due[1:]:
                multiply_tile(*group_and_tile)
            due = []
        g = GROUPS - 1
        step = vector_steps(g)
        step["top_a"]()
        step["mask2"](0)
        step["top_b"]()
        step["mask2"](1)
        quantise(g - 1, "2")
        quantise(g - 1, "13")
        open_tile(g - 1, 0)
        run_passes(g - 1, 0, PASSES, range(8))
        step["mask1"]()
        count_hits(g)
        run_passes(g - 1, 0, PASSES, range(8, 10))
        rows_and_store(g - 1, 0)
        step["count2"]()
        step["product3"]()
        transpose_slot(g, "13", 0)
        step["inverse2"]()
        step["grad_share2"]()
        step["product2"]()
        transpose_slot(g, "2", 0)
        transpose_slot(g, "2", 1)
        step["grad_share1"]()
        step["product1"](0, 1)
        transpose_slot(g, "13", 1)
        step["product1"](1, 2)
        transpose_slot(g, "13", 2)
        transpose_slot(g, "13", 3)
        quantise(g, "2")
        open_tile(g, 0)
        run_passes(g, 0, LAST_PASSES, (0, 1, 2, 3))
        quantise(g, "13", 0, 2)
        run_passes(g, 0, LAST_PASSES, (4, 5, 6, 7))
        empty_row(g, 0, 0, nc.scalar.copy)
        quantise(g, "13", 2, 2)
        run_passes(g, 0, LAST_PASSES, (8, 9))
        empty_row(g, 0, 1, nc.vector.tensor_copy)
        empty_row(g, 0, 2, nc.scalar.copy)
        store_behind(g, 0)
